import numpy as np
import ml_dtypes


def mxq(x, axis, fmt="e4m3"):
    dtype, down = {"e4m3": (ml_dtypes.float8_e4m3fn, 7), "e5m2": (ml_dtypes.float8_e5m2, 14)}[fmt]
    v = np.moveaxis(np.asarray(x, np.float32).astype(ml_dtypes.bfloat16).astype(np.float64), axis, -1)
    blocks = v.reshape(v.shape[:-1] + (-1, 32))
    amax = np.abs(blocks).max(-1, keepdims=True)
    byte = np.maximum(np.where(amax > 0, np.frexp(amax)[1] - 1 + 127, 0) - down, 1)
    scale = np.exp2(byte - 127.0)
    codes = (blocks / scale).astype(np.float32).astype(dtype).astype(np.float64)
    return np.moveaxis((codes * scale).reshape(v.shape), -1, axis)


WIDE = False


def mx_kscale(k):
    if not WIDE:
        return np.ones(k)
    levels = np.array([18, -18])
    if k % 512:
        return np.exp2(np.random.permutation(np.resize(levels, k // 32))).repeat(32)
    a = np.empty((k // 512, 16))
    for p in range(k // 512):
        a[p, :8] = np.random.permutation(np.resize(levels, 8))
        for g in range(8):
            far = levels[np.abs(levels - a[p, g]) >= 10]
            a[p, g + 8] = far[np.random.randint(len(far))]
    return np.exp2(a.ravel()).repeat(32)


BF16 = ml_dtypes.bfloat16


def bf(x):
    return np.asarray(x, np.float32).astype(BF16)


def f64(x):
    return np.asarray(x).astype(np.float64)


B, IN, OUT, NK, DEG = 1024, 256, 1024, 10, 3
K0 = NK + DEG
JIT = 0.25


def b_spline_basis(v, t, degree):
    ve = v[..., None]
    basis = ((ve >= t[:-1]) & (ve < t[1:])).astype(np.float64)
    low = basis
    for p in range(1, degree + 1):
        low = basis
        ti = t[: K0 - p]
        tip = t[p:K0]
        ti1 = t[1 : K0 - p + 1]
        tip1 = t[p + 1 : K0 + 1]
        basis = (ve - ti) / (tip - ti) * low[..., :-1] + (tip1 - ve) / (tip1 - ti1) * low[..., 1:]
    return low, basis


def setup_inputs():
    s = mx_kscale(B)[:, None]
    u = mx_kscale(OUT)
    down = np.where(s < 1.0, s, 1.0)
    gx = np.where(s < 1.0, 0.125 * np.cbrt(s), 1.0)
    knots = np.linspace(0.0, 1.0, K0 + 1)
    knots[1:-1] += np.random.uniform(-JIT, JIT, K0 - 1) / K0
    x = np.random.uniform(0.0, 1.0, (B, IN)) * gx
    cp = np.random.standard_normal((OUT, IN, K0)) * 1.5 / np.sqrt(IN)
    g = np.random.standard_normal((B, OUT)) * np.exp2(np.random.randint(-6, 1, (B, 1)))
    return {"x": bf(x), "knots": bf(knots), "control_points": bf(cp / u[:, None, None]), "grad_out": bf(g / down * u)}


def reference(x, knots, control_points, grad_out):
    t = f64(knots)
    g = f64(grad_out)
    low, basis = b_spline_basis(f64(x), t, DEG)
    slope = DEG / (t[DEG:K0] - t[:NK]) * low[..., :-1] - DEG / (t[DEG + 1 : K0 + 1] - t[1 : NK + 1]) * low[..., 1:]
    w = f64(control_points)[:, :, :NK].reshape(OUT, IN * NK)
    p = mxq(g, 1, "e5m2") @ mxq(w, 0, "e4m3")
    dx = np.sum(slope * p.reshape(B, IN, NK), axis=2)
    a = basis.reshape(B, IN * NK)
    d = mxq(g, 0, "e5m2").T @ mxq(a, 0, "e4m3")
    dcp = np.concatenate([d.reshape(OUT, IN, NK), np.zeros((OUT, IN, DEG))], axis=2)
    return dx, dcp

@@ -1,0 +1,421 @@
+from contextlib import ExitStack
+
+import concourse.mybir as mybir
+from concourse.masks import make_identity
+
+B, IN, OUT, NK, SLOTS = 1024, 256, 1024, 10, 13
+FLOPS = 2 * 2 * B * OUT * IN * NK
+
+F32 = mybir.dt.float32
+BF16 = mybir.dt.bfloat16
+U32 = mybir.dt.uint32
+U8 = mybir.dt.uint8
+E4M3 = mybir.dt.float8_e4m3fn_x4
+E5M2 = mybir.dt.float8_e5m2_x4
+ALU = mybir.AluOpType
+ACT = mybir.ActivationFunctionType
+
+P = 128
+PACK = 4
+PASS = P * PACK
+NQ = NK + 1
+NKNOT = SLOTS + 1
+JC = 32
+NCHUNK = P // JC
+KGROUPS = ((0, 4), (4, 4), (8, 2))
+LAG = 5
+CP_ON_V = ()
+GF_ON_V = (0, 1)
+DCP_ON_V = (3,)
+
+
+def tile_kanlayer_v_kernel(tc, x, knots, control_points, grad_out, out_0, out_1):
+    nc = tc.nc
+    with ExitStack() as ctx:
+        keep = ctx.enter_context(tc.tile_pool(name="keep", bufs=1))
+        work = ctx.enter_context(tc.tile_pool(name="work", bufs=2))
+        psum = ctx.enter_context(tc.psum_pool(name="psum", bufs=2))
+        ctx.enter_context(tc.manual_schedule())
+
+        knots_bf = keep.tile([P, NKNOT], BF16, name="knots_bf")
+        nc.scalar.dma_start(out=knots_bf[:], in_=knots.partition_broadcast(P))
+        x_raw = work.tile([P, 2, PACK, IN], BF16, name="x_raw", tag="tilt")
+        nc.sync.dma_start(out=x_raw[:], in_=x.rearrange("(g p t) j -> p g t j", g=2, t=PACK))
+        g_raw = []
+        for g in range(2):
+            tl = work.tile([P, PACK, OUT], BF16, name="g_raw", tag="io", bufs=3)
+            nc.sync.dma_start(out=tl[:], in_=grad_out[g * PASS:(g + 1) * PASS, :].rearrange("(p t) o -> p t o", t=PACK))
+            g_raw.append(tl)
+        cp_raw = {}
+
+        def load_cp(jh, h):
+            tl = work.tile([P, PACK, P, SLOTS], BF16, name="cp_raw", tag="cp_raw")
+            src = control_points[h * PASS:(h + 1) * PASS, jh * P:(jh + 1) * P, :]
+            nc.sync.dma_start(out=tl[:], in_=src.rearrange("(p t) j k -> p t j k", t=PACK))
+            cp_raw[jh, h] = tl
+
+        load_cp(0, 0)
+        load_cp(0, 1)
+
+        ident_bf = keep.tile([P, P], BF16, name="ident_bf")
+        make_identity(nc, ident_bf[:])
+        ident = keep.tile([P, P], F32, name="ident")
+        make_identity(nc, ident[:])
+
+        def small(name, n):
+            tl = keep.tile([P, n], F32, name=name)
+            return tl
+
+        def tt(name, a, b, op):
+            o = small(name, a.shape[1])
+            nc.vector.tensor_tensor(out=o[:], in0=a, in1=b, op=op)
+            return o
+
+        def scaled(name, a, c):
+            o = small(name, a.shape[1])
+            nc.vector.tensor_scalar(out=o[:], in0=a, scalar1=c, scalar2=None, op0=ALU.mult)
+            return o
+
+        def recip(name, a):
+            o = small(name, a.shape[1])
+            nc.vector.reciprocal(out=o[:], in_=a)
+            return o
+
+        ones = small("ones", NK)
+        nc.vector.memset(ones[:], 1.0)
+        lam = small("lam", NQ)
+        nc.vector.memset(lam[:, 0:1], 1.0)
+        warm = small("warm", 1)
+        nc.scalar.activation(out=warm[:], in_=ones[:, 0:1], func=ACT.Square)
+        t = small("t", NKNOT)
+        nc.vector.tensor_copy(out=t[:], in_=knots_bf[:])
+        neg_t = scaled("neg_t", knots_bf[:], -1.0)
+        d1 = tt("d1", t[:, 1:NKNOT], t[:, 0:NKNOT - 1], ALU.subtract)
+        d2 = tt("d2", t[:, 2:NKNOT], t[:, 0:NKNOT - 2], ALU.subtract)
+        d3 = tt("d3", t[:, 3:NKNOT], t[:, 0:NKNOT - 3], ALU.subtract)
+        d4 = tt("d4", t[:, 4:NKNOT], t[:, 0:NKNOT - 4], ALU.subtract)
+        h_mid = d1[:, 1:NQ + 1]
+        sig = tt("sig", d2[:, :NQ], d2[:, 1:], ALU.add)
+        d2d2 = tt("d2d2", d2[:, :NQ], d2[:, 1:], ALU.mult)
+        hd = tt("hd", h_mid, d2[:, 1:], ALU.mult)
+        hh = tt("hh", d1[:, :NQ], d1[:, 2:], ALU.mult)
+        nc.vector.tensor_tensor_scan(out=lam[:, 1:], data0=d4[:], data1=ones[:], initial=1.0, op0=ALU.mult, op1=ALU.mult)
+        inv_sig = recip("inv_sig", sig[:])
+        prd = tt("prd", d2d2[:], h_mid, ALU.mult)
+        sig_h = tt("sig_h", sig[:], h_mid, ALU.subtract)
+        hh2 = tt("hh2", hh[:], hh[:], ALU.mult)
+        peak = tt("peak", hd[:], inv_sig[:], ALU.mult)
+        inv_sig2 = tt("inv_sig2", inv_sig[:], inv_sig[:], ALU.mult)
+        kap_num = tt("kap_num", sig_h[:], prd[:], ALU.mult)
+        den = tt("den", prd[:], d3[:], ALU.mult)
+        neg_mu = tt("neg_mu", neg_t[:, 1:NQ + 1], peak[:], ALU.subtract)
+        lam_sig = tt("lam_sig", lam[:], sig[:], ALU.mult)
+        kappa = tt("kappa", kap_num[:], inv_sig2[:], ALU.mult)
+        den2 = tt("den2", den[:], hh2[:], ALU.mult)
+        inv_d4 = recip("inv_d4", d4[:])
+        inv_lam = recip("inv_lam", lam[:, :NK])
+        inv_den = recip("inv_den", den2[:])
+        neg_inv_d4 = scaled("neg_inv_d4", inv_d4[:], -1.0)
+        basis_scale = scaled("basis_scale", inv_lam[:], -1.0)
+        gain = tt("gain", lam_sig[:], inv_den[:], ALU.mult)
+        slope_scale = scaled("slope_scale", inv_lam[:], -3.0)
+
+        def mx_pair(name, width):
+            codes = keep.tile([P, width], U32, name=name + "_codes", align_bytes=64)
+            scales = keep.tile([P, width], U8, name=name + "_scales", align_bytes=64)
+            return codes, scales
+
+        g_feat = [mx_pair("g_feat%d" % h, B) for h in range(2)]
+        g_tok = [mx_pair("g_tok%d" % g, OUT) for g in range(2)]
+        cp_mx = {(jh, h): mx_pair("cp%d%d" % (jh, h), NK * P) for jh in range(2) for h in range(2)}
+        basis_mx = [mx_pair("basis%d" % g, NCHUNK * PASS) for g in range(2)]
+        basis_bf = []
+        for g in range(2):
+            tl = keep.tile([P, NCHUNK, NK, JC, PACK], BF16, name="basis_bf%d" % g, align_bytes=64)
+            basis_bf.append(tl)
+            codes, scales = basis_mx[g]
+            nc.gpsimd.memset(codes[:].rearrange("p (c w) -> p c w", c=NCHUNK)[:, :, NK * JC:], 0)
+            nc.gpsimd.memset(scales[:].bitcast(U32), 0)
+
+        x_t = []
+        for jh in range(2):
+            tl = keep.tile([P, 2, PASS], BF16, name="x_t%d" % jh)
+            for g in range(2):
+                bank = psum.tile([P, PACK, P], BF16, name="xt_bank", tag="basis")
+                for tk in range(PACK):
+                    nc.tensor.transpose(bank[:, tk, :], x_raw[:, g, tk, jh * P:(jh + 1) * P], ident_bf[:])
+                nc.scalar.copy(out=tl[:, g, :], in_=bank[:].rearrange("p t q -> p (t q)"))
+            x_t.append(tl[:].rearrange("p g n -> p (g n)"))
+
+        pending = []
+
+        def new_stage():
+            st = work.tile([P, PACK * PASS], BF16, name="stage", tag="stage", bufs=3, align_bytes=64)
+            return st
+
+        def quantise_pending():
+            for st, (codes, scales), c0, n, fmt in pending:
+                nc.vector.quantize_mx(out=codes[:, c0:c0 + n].bitcast(fmt), scales=scales[:, c0:c0 + n], in_=st[:, :PACK * n])
+            pending.clear()
+
+        def make_g_feat(h, g, tags, on_vector):
+            st = new_stage()
+            words = st[:].bitcast(F32).rearrange("p (t q u) -> p t q u", t=PACK, u=2)
+            for half in range(2):
+                bank = psum.tile([P, 2, 2, P], F32, name="gt_bank", tag=tags)
+                for t2 in range(2):
+                    src = g_raw[g][:, 2 * half + t2, :].bitcast(F32)
+                    for u in range(2):
+                        nc.tensor.transpose(bank[:, t2, u, :], src[:, 256 * h + u:256 * (h + 1):2], ident[:])
+                copy = nc.vector.tensor_copy if on_vector and half == 1 else nc.scalar.copy
+                copy(out=words[:, 2 * half:2 * half + 2, :, :], in_=bank[:].rearrange("p t u q -> p t q u"))
+            pending.append((st, g_feat[h], g * PASS, PASS, E5M2))
+
+        def make_g_tok(g, half):
+            st = new_stage()
+            src = g_raw[g][:, :, half * PASS:(half + 1) * PASS]
+            nc.vector.tensor_copy(out=st[:].rearrange("p (c i t) -> p c t i", i=4, t=PACK),
+                                  in_=src.rearrange("p t (c i) -> p c t i", i=4))
+            pending.append((st, g_tok[g], half * PASS, PASS, E5M2))
+
+        def make_cp(jh, h, kg):
+            k0, nk = KGROUPS[kg]
+            st = new_stage()
+            copy = nc.vector.tensor_copy if (jh, h, kg) in CP_ON_V else nc.scalar.copy
+            copy(out=st[:, :nk * PASS].rearrange("p (k j t) -> p j t k", k=nk, t=PACK),
+                           in_=cp_raw[jh, h][:, :, :, k0:k0 + nk].rearrange("p t j k -> p j t k"))
+            pending.append((st, cp_mx[jh, h], k0 * P, nk * P, E4M3))
+
+        clamped, squares, quad, slope, tilt, p_bank, b_bank, dx_bank = {}, {}, {}, {}, {}, {}, {}, {}
+
+        def clamp(q):
+            jh, m = divmod(q, NQ)
+            for i in (range(3) if m == 0 else [m + 2]):
+                c = work.tile([P, B], BF16, name="clamped", tag="clamped", bufs=5)
+                nc.vector.tensor_scalar(out=c[:], in0=x_t[jh], scalar1=t[:, i:i + 1], scalar2=t[:, i + 1:i + 2],
+                                        op0=ALU.max, op1=ALU.min)
+                clamped[jh, i] = c
+
+        def square(q, piece):
+            jh, m = divmod(q, NQ)
+            tag, bias = (("rise", neg_t[:, m:m + 1]), ("mid", neg_mu[:, m:m + 1]), ("fall", neg_t[:, m + 3:m + 4]))[piece]
+            s = work.tile([P, B], F32, name=tag, tag=tag)
+            nc.scalar.activation(out=s[:], in_=clamped[jh, m + piece][:], func=ACT.Square, bias=bias)
+            squares[q, piece] = s
+
+        def quad_first(q):
+            m = q % NQ
+            rise, mid, fall = squares[q, 0], squares[q, 1], squares.get((q, 2))
+            nc.vector.scalar_tensor_tensor(out=mid[:], in0=mid[:], scalar=kappa[:, m:m + 1], in1=rise[:],
+                                           op0=ALU.subtract, op1=ALU.mult)
+
+        def quad_second(q):
+            m = q % NQ
+            rise, mid, fall = squares[q, 0], squares[q, 1], squares.get((q, 2))
+            w = work.tile([P, B], F32, name="quad", tag="quad", bufs=3)
+            nc.vector.scalar_tensor_tensor(out=w[:], in0=mid[:], scalar=gain[:, m:m + 1], in1=fall[:],
+                                           op0=ALU.mult, op1=ALU.mult)
+            quad[q] = w
+
+        def make_slope(q):
+            k = q % NQ
+            s = work.tile([P, B], F32, name="slope", tag="slope", bufs=LAG - 1)
+            nc.vector.scalar_tensor_tensor(out=s[:], in0=quad[q + 1][:], scalar=neg_inv_d4[:, k:k + 1], in1=quad[q][:],
+                                           op0=ALU.mult, op1=ALU.add)
+            slope[q] = s
+
+        def make_tilt(q):
+            jh, k = divmod(q, NQ)
+            s = work.tile([P, B], F32, name="tilt", tag="tilt")
+            nc.vector.scalar_tensor_tensor(out=s[:], in0=x_t[jh], scalar=t[:, k:k + 1], in1=slope[q][:],
+                                           op0=ALU.subtract, op1=ALU.mult)
+            tilt[q] = s
+
+        def basis_sum(q):
+            for g in range(2):
+                bank = psum.tile([P, PACK, P], F32, name="b_bank", tag="basis")
+                for tk in range(PACK):
+                    cols = slice(g * PASS + tk * P, g * PASS + (tk + 1) * P)
+                    nc.tensor.matmul(bank[:, tk, :], lhsT=quad[q + 1][:, cols], rhs=ident[:], is_transpose=True, start=True, stop=False)
+                    nc.tensor.matmul(bank[:, tk, :], lhsT=tilt[q][:, cols], rhs=ident[:], is_transpose=True, start=False, stop=True)
+                b_bank[q, g] = bank
+
+        def basis_round(q):
+            k = q % NQ
+            for g in range(2):
+                nc.scalar.activation(out=basis_bf[g][:, :, k, :, :],
+                                     in_=b_bank[q, g][:].rearrange("p t (c j) -> p c j t", c=NCHUNK),
+                                     func=ACT.Copy, scale=basis_scale[:, k:k + 1])
+
+        def basis_quantise(k0, nk):
+            for c in range(NCHUNK):
+                for g in range(2):
+                    codes, scales = basis_mx[g]
+                    cols = slice(c * PASS + k0 * JC, c * PASS + (k0 + nk) * JC)
+                    nc.vector.quantize_mx(out=codes[:, cols].bitcast(E4M3), scales=scales[:, cols],
+                                          in_=basis_bf[g][:, c, k0:k0 + nk, :, :].rearrange("p k j t -> p (k j t)"))
+
+        def p_matmuls(q):
+            jh, k = divmod(q, NQ)
+            for g in range(2):
+                bank = psum.tile([P, PASS], F32, name="p_bank", tag="p")
+                for h in range(2):
+                    wc, ws = cp_mx[jh, h]
+                    gc, gs = g_feat[h]
+                    nc.tensor.matmul_mx(out=bank[:], lhsT=wc[:, k * P:(k + 1) * P].bitcast(E4M3), lhsT_scale=ws[:, k * P:(k + 1) * P],
+                                        rhs=gc[:, g * PASS:(g + 1) * PASS].bitcast(E5M2), rhs_scale=gs[:, g * PASS:(g + 1) * PASS],
+                                        start=(h == 0), stop=(h == 1))
+                p_bank[q, g] = bank
+
+        prods = {}
+
+        def dx_term(q, g):
+            jh, k = divmod(q, NQ)
+            prod = work.tile([P, PASS], F32, name="prod", tag="prod", bufs=3)
+            nc.vector.scalar_tensor_tensor(out=prod[:], in0=slope[q][:, g * PASS:(g + 1) * PASS], scalar=slope_scale[:, k:k + 1],
+                                           in1=p_bank[q, g][:], op0=ALU.mult, op1=ALU.mult)
+            prods[q, g] = prod
+
+        def dx_flip(q, g):
+            jh, k = divmod(q, NQ)
+            prod = prods[q, g]
+            if k == 0:
+                bank = psum.tile([P, PACK, P], F32, name="dx_bank", tag="dx")
+                dx_bank[jh, g] = bank
+            for tk in range(PACK):
+                nc.tensor.matmul(dx_bank[jh, g][:, tk, :], lhsT=prod[:, tk * P:(tk + 1) * P], rhs=ident[:], is_transpose=True,
+                                 start=(k == 0 and tk == 0), stop=(k == NK - 1 and tk == PACK - 1))
+
+        def dx_store(jh):
+            for g in range(2):
+                res = work.tile([P, PACK, P], F32, name="dx_res", tag="dx_res")
+                nc.scalar.copy(out=res[:], in_=dx_bank[jh, g][:])
+                dst = out_0[g * PASS:(g + 1) * PASS, jh * P:(jh + 1) * P]
+                nc.sync.dma_start(out=dst.rearrange("(p t) j -> p t j", t=PACK), in_=res[:])
+
+        dcp_res, o_bank = {}, {}
+
+        def dcp_matmuls(jh, u, tag):
+            ot, c = divmod(u, NCHUNK)
+            bank = psum.tile([P, PASS], F32, name="o_bank", tag=tag)
+            for g in range(2):
+                gc, gs = g_tok[g]
+                bc, bs = basis_mx[g]
+                nc.tensor.matmul_mx(out=bank[:], lhsT=gc[:, ot * P:(ot + 1) * P].bitcast(E5M2), lhsT_scale=gs[:, ot * P:(ot + 1) * P],
+                                    rhs=bc[:, c * PASS:(c + 1) * PASS].bitcast(E4M3), rhs_scale=bs[:, c * PASS:(c + 1) * PASS],
+                                    start=(g == 0), stop=(g == 1))
+            o_bank[jh, u] = bank
+
+        def dcp_copy(jh, u, copy):
+            ot, c = divmod(u, NCHUNK)
+            if c == 0:
+                if jh == 1 and ot % 2 == 1:
+                    res = work.tile([P, P, SLOTS], F32, name="dcp_res", tag="cp_raw")
+                else:
+                    res = work.tile([P, P, SLOTS], F32, name="dcp_res", tag="io", bufs=3)
+                dcp_res[jh, ot] = res
+            res = dcp_res[jh, ot]
+            copy(out=res[:, c * JC:(c + 1) * JC, :], in_=o_bank[jh, u][:, :SLOTS * JC].rearrange("p (k j) -> p j k", j=JC))
+            if c == NCHUNK - 1:
+                nc.sync.dma_start(out=out_1[ot * P:(ot + 1) * P, jh * P:(jh + 1) * P, :], in_=res[:])
+
+        def dx_q(n):
+            i = n - LAG
+            return i + i // NK if 0 <= i < 2 * NK else -1
+
+        def is_quad(q):
+            return 0 <= q < 2 * NQ
+
+        def is_cubic(q):
+            return is_quad(q) and q % NQ < NK
+
+        units = OUT // P * NCHUNK
+
+        def dcp_pair(u):
+            for v in (u, u + 1):
+                if 0 <= v < units:
+                    dcp_copy(0, v, nc.vector.tensor_copy if v % 8 in DCP_ON_V else nc.scalar.copy)
+            for v in (u + 2, u + 3):
+                if 0 <= v < units:
+                    dcp_matmuls(0, v, "out")
+
+        clamp(0)
+        for piece in range(3):
+            square(0, piece)
+        clamp(1)
+        last_basis = 2 * NQ - 2 + 3
+        first_dcp = NK + 3
+        for n in range(last_basis):
+            u0 = NCHUNK * (n - first_dcp)
+            if is_cubic(n - 3):
+                basis_sum(n - 3)
+            if n == LAG + NK:
+                dx_store(0)
+            if is_cubic(dx_q(n)):
+                dx_term(dx_q(n), 0)
+            if is_quad(n):
+                quad_first(n)
+            dcp_pair(u0 - 2)
+            if is_cubic(dx_q(n)):
+                dx_term(dx_q(n), 1)
+            if is_quad(n + 1):
+                square(n + 1, 0)
+            if is_cubic(n - 3):
+                basis_round(n - 3)
+            if is_cubic(dx_q(n)):
+                dx_flip(dx_q(n), 0)
+                dx_flip(dx_q(n), 1)
+            if is_cubic(dx_q(n + 1)):
+                p_matmuls(dx_q(n + 1))
+            if is_cubic(n - 2):
+                make_slope(n - 2)
+            if is_quad(n + 2):
+                clamp(n + 2)
+            if is_quad(n):
+                quad_second(n)
+            dcp_pair(u0)
+            if is_quad(n + 1):
+                square(n + 1, 1)
+                square(n + 1, 2)
+            quantise_pending()
+            if is_cubic(n - 2):
+                make_tilt(n - 2)
+            if is_cubic(n - 3) and (n - 3) % NQ == 7:
+                basis_quantise(0, 8)
+            if n - 3 == NK - 1:
+                basis_quantise(8, 2)
+            if n < 2:
+                make_g_feat(0, n, "out", n in GF_ON_V)
+                make_g_feat(1, n, "p", n in GF_ON_V)
+            if 1 <= n < 7:
+                make_cp(0, (n - 1) % 2, (n - 1) // 2)
+            if n in (5, 6):
+                load_cp(1, n - 5)
+            if 7 <= n < 13:
+                make_cp(1, (n - 7) % 2, (n - 7) // 2)
+            if 4 <= n < 8:
+                make_g_tok((n - 4) // 2, n % 2)
+        basis_sum(last_basis - 3)
+        basis_round(last_basis - 3)
+        q = dx_q(last_basis)
+        dx_term(q, 0)
+        dx_term(q, 1)
+        dx_flip(q, 0)
+        dx_flip(q, 1)
+        p_matmuls(q + 1)
+        basis_quantise(8, 2)
+        tags = ("out", "out", "basis", "basis")
+        for u in range(NCHUNK):
+            dcp_matmuls(1, u, tags[u])
+        for u in range(units):
+            ot, c = divmod(u, NCHUNK)
+            dcp_copy(1, u, nc.scalar.copy if u % 2 == 0 else nc.vector.tensor_copy)
+            if u + NCHUNK < units:
+                dcp_matmuls(1, u + NCHUNK, tags[c])
+            if u in (1, 3):
+                dx_term(q + 1, u // 2)
+            if u == 5:
+                dx_flip(q + 1, 0)
+                dx_flip(q + 1, 1)
+            if u == 7:
+                dx_store(1)

@@ -26,7 +26,8 @@ KGROUPS = ((0, 4), (4, 4), (8, 2))
 LAG = 5
 CP_ON_V = ()
 GF_ON_V = (0, 1)
-DCP_ON_V = (3,)
+DCP_ON_V = (0, 1, 4, 5)
+G_COLS = 832
 
 
 def tile_kanlayer_v_kernel(tc, x, knots, control_points, grad_out, out_0, out_1):
@@ -49,7 +50,7 @@ def tile_kanlayer_v_kernel(tc, x, knots, control_points, grad_out, out_0, out_1)
         cp_raw = {}
 
         def load_cp(jh, h):
-            tl = work.tile([P, PACK, P, SLOTS], BF16, name="cp_raw", tag="cp_raw")
+            tl = work.tile([P, PACK, P, SLOTS], BF16, name="cp_raw", tag="cp_raw", align_bytes=64)
             src = control_points[h * PASS:(h + 1) * PASS, jh * P:(jh + 1) * P, :]
             nc.sync.dma_start(out=tl[:], in_=src.rearrange("(p t) j k -> p t j k", t=PACK))
             cp_raw[jh, h] = tl
@@ -86,39 +87,34 @@ def tile_kanlayer_v_kernel(tc, x, knots, control_points, grad_out, out_0, out_1)
         lam = small("lam", NQ)
         nc.vector.memset(lam[:, 0:1], 1.0)
         warm = small("warm", 1)
-        nc.scalar.activation(out=warm[:], in_=ones[:, 0:1], func=ACT.Square)
+        nc.scalar.activation(out=warm[:], in_=ones[:, 0:1], func=ACT.Sqrt)
         t = small("t", NKNOT)
         nc.vector.tensor_copy(out=t[:], in_=knots_bf[:])
         neg_t = scaled("neg_t", knots_bf[:], -1.0)
         d1 = tt("d1", t[:, 1:NKNOT], t[:, 0:NKNOT - 1], ALU.subtract)
         d2 = tt("d2", t[:, 2:NKNOT], t[:, 0:NKNOT - 2], ALU.subtract)
-        d3 = tt("d3", t[:, 3:NKNOT], t[:, 0:NKNOT - 3], ALU.subtract)
         d4 = tt("d4", t[:, 4:NKNOT], t[:, 0:NKNOT - 4], ALU.subtract)
+        d3 = tt("d3", t[:, 3:NKNOT], t[:, 0:NKNOT - 3], ALU.subtract)
         h_mid = d1[:, 1:NQ + 1]
-        sig = tt("sig", d2[:, :NQ], d2[:, 1:], ALU.add)
         d2d2 = tt("d2d2", d2[:, :NQ], d2[:, 1:], ALU.mult)
-        hd = tt("hd", h_mid, d2[:, 1:], ALU.mult)
         hh = tt("hh", d1[:, :NQ], d1[:, 2:], ALU.mult)
         nc.vector.tensor_tensor_scan(out=lam[:, 1:], data0=d4[:], data1=ones[:], initial=1.0, op0=ALU.mult, op1=ALU.mult)
-        inv_sig = recip("inv_sig", sig[:])
+        sig = tt("sig", d2[:, :NQ], d2[:, 1:], ALU.add)
         prd = tt("prd", d2d2[:], h_mid, ALU.mult)
-        sig_h = tt("sig_h", sig[:], h_mid, ALU.subtract)
         hh2 = tt("hh2", hh[:], hh[:], ALU.mult)
+        hd = tt("hd", h_mid, d2[:, 1:], ALU.mult)
+        den = tt("den", prd[:], d3[:], ALU.mult)
+        lam_sig = tt("lam_sig", lam[:], sig[:], ALU.mult)
+        inv_sig = recip("inv_sig", sig[:])
+        den2 = tt("den2", den[:], hh2[:], ALU.mult)
+        sig_h = tt("sig_h", sig[:], h_mid, ALU.subtract)
         peak = tt("peak", hd[:], inv_sig[:], ALU.mult)
+        inv_den = recip("inv_den", den2[:])
         inv_sig2 = tt("inv_sig2", inv_sig[:], inv_sig[:], ALU.mult)
         kap_num = tt("kap_num", sig_h[:], prd[:], ALU.mult)
-        den = tt("den", prd[:], d3[:], ALU.mult)
-        neg_mu = tt("neg_mu", neg_t[:, 1:NQ + 1], peak[:], ALU.subtract)
-        lam_sig = tt("lam_sig", lam[:], sig[:], ALU.mult)
-        kappa = tt("kappa", kap_num[:], inv_sig2[:], ALU.mult)
-        den2 = tt("den2", den[:], hh2[:], ALU.mult)
-        inv_d4 = recip("inv_d4", d4[:])
-        inv_lam = recip("inv_lam", lam[:, :NK])
-        inv_den = recip("inv_den", den2[:])
-        neg_inv_d4 = scaled("neg_inv_d4", inv_d4[:], -1.0)
-        basis_scale = scaled("basis_scale", inv_lam[:], -1.0)
         gain = tt("gain", lam_sig[:], inv_den[:], ALU.mult)
-        slope_scale = scaled("slope_scale", inv_lam[:], -3.0)
+        neg_mu = tt("neg_mu", neg_t[:, 1:NQ + 1], peak[:], ALU.subtract)
+        kappa1 = tt("kappa1", kap_num[:], inv_sig2[:], ALU.mult)
 
         def mx_pair(name, width):
             codes = keep.tile([P, width], U32, name=name + "_codes", align_bytes=64)
@@ -128,24 +124,31 @@ def tile_kanlayer_v_kernel(tc, x, knots, control_points, grad_out, out_0, out_1)
         g_feat = [mx_pair("g_feat%d" % h, B) for h in range(2)]
         g_tok = [mx_pair("g_tok%d" % g, OUT) for g in range(2)]
         cp_mx = {(jh, h): mx_pair("cp%d%d" % (jh, h), NK * P) for jh in range(2) for h in range(2)}
-        basis_mx = [mx_pair("basis%d" % g, NCHUNK * PASS) for g in range(2)]
+        basis_mx = {(0, g): mx_pair("basis%d" % g, NCHUNK * PASS) for g in range(2)}
+
+        def zero_fill(jh, g):
+            codes, scales = basis_mx[0, g]
+            nc.gpsimd.memset(codes[:].rearrange("p (c w) -> p c w", c=NCHUNK)[:, :, NK * JC:], 0)
+            nc.gpsimd.memset(scales[:].bitcast(U32).rearrange("p (c w) -> p c w", c=NCHUNK)[:, :, NK * JC // 4:], 0)
+
         basis_bf = []
         for g in range(2):
             tl = keep.tile([P, NCHUNK, NK, JC, PACK], BF16, name="basis_bf%d" % g, align_bytes=64)
             basis_bf.append(tl)
-            codes, scales = basis_mx[g]
-            nc.gpsimd.memset(codes[:].rearrange("p (c w) -> p c w", c=NCHUNK)[:, :, NK * JC:], 0)
-            nc.gpsimd.memset(scales[:].bitcast(U32), 0)
+            zero_fill(0, g)
 
-        x_t = []
+        x_t, x_bank = [], []
         for jh in range(2):
-            tl = keep.tile([P, 2, PASS], BF16, name="x_t%d" % jh)
+            tl = keep.tile([P, B], BF16, name="x_t%d" % jh)
+            bank = psum.tile([P, 2, PACK, P], BF16, name="xt_bank", tag=("out", "basis")[jh])
             for g in range(2):
-                bank = psum.tile([P, PACK, P], BF16, name="xt_bank", tag="basis")
                 for tk in range(PACK):
-                    nc.tensor.transpose(bank[:, tk, :], x_raw[:, g, tk, jh * P:(jh + 1) * P], ident_bf[:])
-                nc.scalar.copy(out=tl[:, g, :], in_=bank[:].rearrange("p t q -> p (t q)"))
-            x_t.append(tl[:].rearrange("p g n -> p (g n)"))
+                    nc.tensor.transpose(bank[:, g, tk, :], x_raw[:, g, tk, jh * P:(jh + 1) * P], ident_bf[:])
+            x_bank.append(bank[:].rearrange("p g t q -> p (g t q)"))
+            x_t.append(tl[:])
+        nc.scalar.copy(out=x_t[0], in_=x_bank[0])
+        root0 = small("root0", NQ)
+        nc.scalar.activation(out=root0[:], in_=gain[:], func=ACT.Sqrt)
 
         pending = []
 
@@ -167,24 +170,34 @@ def tile_kanlayer_v_kernel(tc, x, knots, control_points, grad_out, out_0, out_1)
                     src = g_raw[g][:, 2 * half + t2, :].bitcast(F32)
                     for u in range(2):
                         nc.tensor.transpose(bank[:, t2, u, :], src[:, 256 * h + u:256 * (h + 1):2], ident[:])
-                copy = nc.vector.tensor_copy if on_vector and half == 1 else nc.scalar.copy
+                copy = nc.vector.tensor_copy if half == 1 else nc.scalar.copy
                 copy(out=words[:, 2 * half:2 * half + 2, :, :], in_=bank[:].rearrange("p t u q -> p t q u"))
             pending.append((st, g_feat[h], g * PASS, PASS, E5M2))
 
-        def make_g_tok(g, half):
+        def make_g_tok(g, quarter):
             st = new_stage()
-            src = g_raw[g][:, :, half * PASS:(half + 1) * PASS]
-            nc.vector.tensor_copy(out=st[:].rearrange("p (c i t) -> p c t i", i=4, t=PACK),
+            width = OUT // 4
+            src = g_raw[g][:, :, quarter * width:(quarter + 1) * width]
+            copy = nc.vector.tensor_copy if True else nc.scalar.copy
+            copy(out=st[:, :PACK * width].rearrange("p (c i t) -> p c t i", i=4, t=PACK),
                                   in_=src.rearrange("p t (c i) -> p c t i", i=4))
-            pending.append((st, g_tok[g], half * PASS, PASS, E5M2))
+            pending.append((st, g_tok[g], quarter * width, width, E5M2))
 
-        def make_cp(jh, h, kg):
-            k0, nk = KGROUPS[kg]
-            st = new_stage()
-            copy = nc.vector.tensor_copy if (jh, h, kg) in CP_ON_V else nc.scalar.copy
-            copy(out=st[:, :nk * PASS].rearrange("p (k j t) -> p j t k", k=nk, t=PACK),
-                           in_=cp_raw[jh, h][:, :, :, k0:k0 + nk].rearrange("p t j k -> p j t k"))
-            pending.append((st, cp_mx[jh, h], k0 * P, nk * P, E4M3))
+        cp_units = [(jh, h, k0, nk, j0, nj) for jh in range(2) for k0, nk in KGROUPS for h in range(2)
+                    for nj in [2 * P // nk] for j0 in range(0, P, nj)]
+        cp_stage = {}
+
+        def make_cp(i):
+            jh, h, k0, nk, j0, nj = cp_units[i]
+            if j0 == 0:
+                cp_stage[jh, h, k0] = new_stage()
+            st = cp_stage[jh, h, k0]
+            nc.scalar.copy(out=st[:, :nk * PASS].rearrange("p (k j t) -> p j t k", k=nk, t=PACK)[:, j0:j0 + nj, :, :],
+                           in_=cp_raw[jh, h][:, :, j0:j0 + nj, k0:k0 + nk].rearrange("p t j k -> p j t k"))
+            if j0 + nj == P:
+                pending.append((st, cp_mx[jh, h], k0 * P, nk * P, E4M3))
+            if jh == 0 and k0 + nk == NK:
+                load_cp(1, h)
 
         clamped, squares, quad, slope, tilt, p_bank, b_bank, dx_bank = {}, {}, {}, {}, {}, {}, {}, {}
 
@@ -198,9 +211,13 @@ def tile_kanlayer_v_kernel(tc, x, knots, control_points, grad_out, out_0, out_1)
 
         def square(q, piece):
             jh, m = divmod(q, NQ)
-            tag, bias = (("rise", neg_t[:, m:m + 1]), ("mid", neg_mu[:, m:m + 1]), ("fall", neg_t[:, m + 3:m + 4]))[piece]
-            s = work.tile([P, B], F32, name=tag, tag=tag)
-            nc.scalar.activation(out=s[:], in_=clamped[jh, m + piece][:], func=ACT.Square, bias=bias)
+            s = work.tile([P, B], F32, name="square", tag=("rise", "mid", "fall")[piece])
+            if piece == 1:
+                nc.scalar.activation(out=s[:], in_=clamped[jh, m + 1][:], func=ACT.Square,
+                                     bias=mid_bias[:, m:m + 1], scale=root[:, m:m + 1])
+            else:
+                knot = m + 3 * (piece // 2)
+                nc.scalar.activation(out=s[:], in_=clamped[jh, m + piece][:], func=ACT.Square, bias=neg_t[:, knot:knot + 1])
             squares[q, piece] = s
 
         def quad_first(q):
@@ -209,17 +226,21 @@ def tile_kanlayer_v_kernel(tc, x, knots, control_points, grad_out, out_0, out_1)
             nc.vector.scalar_tensor_tensor(out=mid[:], in0=mid[:], scalar=kappa[:, m:m + 1], in1=rise[:],
                                            op0=ALU.subtract, op1=ALU.mult)
 
-        def quad_second(q):
-            m = q % NQ
-            rise, mid, fall = squares[q, 0], squares[q, 1], squares.get((q, 2))
-            w = work.tile([P, B], F32, name="quad", tag="quad", bufs=3)
-            nc.vector.scalar_tensor_tensor(out=w[:], in0=mid[:], scalar=gain[:, m:m + 1], in1=fall[:],
-                                           op0=ALU.mult, op1=ALU.mult)
-            quad[q] = w
+        def g_cols(q):
+            return 0 if q < 2 else (384 if q < LAG or q in (12, 13) else G_COLS)
+
+        def quad_second(q, on_gpsimd):
+            engine = nc.gpsimd if on_gpsimd else nc.vector
+            mid, fall = squares[q, 1], squares[q, 2]
+            if on_gpsimd or g_cols(q) == 0:
+                w = work.tile([P, B], F32, name="quad", tag="quad", bufs=3)
+                quad[q] = w
+            cols = slice(0, g_cols(q)) if on_gpsimd else slice(g_cols(q), B)
+            engine.tensor_tensor(out=quad[q][:, cols], in0=mid[:, cols], in1=fall[:, cols], op=ALU.mult)
 
         def make_slope(q):
             k = q % NQ
-            s = work.tile([P, B], F32, name="slope", tag="slope", bufs=LAG - 1)
+            s = work.tile([P, B], F32, name="slope", tag="slope", bufs=4)
             nc.vector.scalar_tensor_tensor(out=s[:], in0=quad[q + 1][:], scalar=neg_inv_d4[:, k:k + 1], in1=quad[q][:],
                                            op0=ALU.mult, op1=ALU.add)
             slope[q] = s
@@ -227,7 +248,7 @@ def tile_kanlayer_v_kernel(tc, x, knots, control_points, grad_out, out_0, out_1)
         def make_tilt(q):
             jh, k = divmod(q, NQ)
             s = work.tile([P, B], F32, name="tilt", tag="tilt")
-            nc.vector.scalar_tensor_tensor(out=s[:], in0=x_t[jh], scalar=t[:, k:k + 1], in1=slope[q][:],
+            nc.vector.scalar_tensor_tensor(out=s[:], in0=(x_bank[0], x_t[1])[jh], scalar=t[:, k:k + 1], in1=slope[q][:],
                                            op0=ALU.subtract, op1=ALU.mult)
             tilt[q] = s
 
@@ -240,17 +261,23 @@ def tile_kanlayer_v_kernel(tc, x, knots, control_points, grad_out, out_0, out_1)
                     nc.tensor.matmul(bank[:, tk, :], lhsT=tilt[q][:, cols], rhs=ident[:], is_transpose=True, start=False, stop=True)
                 b_bank[q, g] = bank
 
-        def basis_round(q):
+        def basis_round(q, on_vector=()):
             k = q % NQ
+            for g in on_vector:
+                nc.vector.tensor_scalar(out=basis_bf[g][:, :, k, :, :],
+                                        in0=b_bank[q, g][:].rearrange("p t (c j) -> p c j t", c=NCHUNK),
+                                        scalar1=basis_scale[:, k:k + 1], scalar2=None, op0=ALU.mult)
             for g in range(2):
+                if g in on_vector:
+                    continue
                 nc.scalar.activation(out=basis_bf[g][:, :, k, :, :],
                                      in_=b_bank[q, g][:].rearrange("p t (c j) -> p c j t", c=NCHUNK),
                                      func=ACT.Copy, scale=basis_scale[:, k:k + 1])
 
-        def basis_quantise(k0, nk):
-            for c in range(NCHUNK):
+        def basis_quantise(jh, k0, nk, chunks=range(NCHUNK)):
+            for c in chunks:
                 for g in range(2):
-                    codes, scales = basis_mx[g]
+                    codes, scales = basis_mx[0, g]
                     cols = slice(c * PASS + k0 * JC, c * PASS + (k0 + nk) * JC)
                     nc.vector.quantize_mx(out=codes[:, cols].bitcast(E4M3), scales=scales[:, cols],
                                           in_=basis_bf[g][:, c, k0:k0 + nk, :, :].rearrange("p k j t -> p (k j t)"))
@@ -300,7 +327,7 @@ def tile_kanlayer_v_kernel(tc, x, knots, control_points, grad_out, out_0, out_1)
             bank = psum.tile([P, PASS], F32, name="o_bank", tag=tag)
             for g in range(2):
                 gc, gs = g_tok[g]
-                bc, bs = basis_mx[g]
+                bc, bs = basis_mx[0, g]
                 nc.tensor.matmul_mx(out=bank[:], lhsT=gc[:, ot * P:(ot + 1) * P].bitcast(E5M2), lhsT_scale=gs[:, ot * P:(ot + 1) * P],
                                     rhs=bc[:, c * PASS:(c + 1) * PASS].bitcast(E4M3), rhs_scale=bs[:, c * PASS:(c + 1) * PASS],
                                     start=(g == 0), stop=(g == 1))
@@ -310,7 +337,7 @@ def tile_kanlayer_v_kernel(tc, x, knots, control_points, grad_out, out_0, out_1)
             ot, c = divmod(u, NCHUNK)
             if c == 0:
                 if jh == 1 and ot % 2 == 1:
-                    res = work.tile([P, P, SLOTS], F32, name="dcp_res", tag="cp_raw")
+                    res = work.tile([P, P, SLOTS], F32, name="dcp_res", tag="cp_raw", align_bytes=64)
                 else:
                     res = work.tile([P, P, SLOTS], F32, name="dcp_res", tag="io", bufs=3)
                 dcp_res[jh, ot] = res
@@ -320,7 +347,7 @@ def tile_kanlayer_v_kernel(tc, x, knots, control_points, grad_out, out_0, out_1)
                 nc.sync.dma_start(out=out_1[ot * P:(ot + 1) * P, jh * P:(jh + 1) * P, :], in_=res[:])
 
         def dx_q(n):
-            i = n - LAG
+            i = n - LAG + (n >= LAG + NK)
             return i + i // NK if 0 <= i < 2 * NK else -1
 
         def is_quad(q):
@@ -331,91 +358,128 @@ def tile_kanlayer_v_kernel(tc, x, knots, control_points, grad_out, out_0, out_1)
 
         units = OUT // P * NCHUNK
 
-        def dcp_pair(u):
-            for v in (u, u + 1):
-                if 0 <= v < units:
-                    dcp_copy(0, v, nc.vector.tensor_copy if v % 8 in DCP_ON_V else nc.scalar.copy)
-            for v in (u + 2, u + 3):
-                if 0 <= v < units:
-                    dcp_matmuls(0, v, "out")
+        started = []
+
+        def dcp_advance(count, copy):
+            for v in range(count):
+                done = len(started) - 2
+                if 0 <= done < units:
+                    dcp_copy(0, done, copy)
+                if len(started) < units:
+                    dcp_matmuls(0, len(started), "out")
+                started.append(v)
 
         clamp(0)
-        for piece in range(3):
-            square(0, piece)
+        square(0, 0)
+        square(0, 2)
+        inv_root0 = recip("inv_root0", root0[:])
+        kappa = tt("kappa", kappa1[:], gain[:], ALU.mult)
+        inv_d4 = recip("inv_d4", d4[:])
+        quot = tt("quot", gain[:], inv_root0[:], ALU.mult)
+        inv_lam = recip("inv_lam", lam[:, :NK])
+        neg_inv_d4 = scaled("neg_inv_d4", inv_d4[:], -1.0)
+        root2 = tt("root2", quot[:], root0[:], ALU.add)
+        basis_scale = scaled("basis_scale", inv_lam[:], -1.0)
+        slope_scale = scaled("slope_scale", inv_lam[:], -3.0)
+        root = scaled("root", root2[:], 0.5)
+        mid_bias = tt("mid_bias", neg_mu[:], root[:], ALU.mult)
+        square(0, 1)
+        nc.scalar.copy(out=x_t[1], in_=x_bank[1])
         clamp(1)
         last_basis = 2 * NQ - 2 + 3
         first_dcp = NK + 3
-        for n in range(last_basis):
+        for n in range(last_basis - 1):
             u0 = NCHUNK * (n - first_dcp)
             if is_cubic(n - 3):
                 basis_sum(n - 3)
-            if n == LAG + NK:
-                dx_store(0)
-            if is_cubic(dx_q(n)):
-                dx_term(dx_q(n), 0)
+            if is_cubic(n - 2):
+                make_slope(n - 2)
             if is_quad(n):
                 quad_first(n)
-            dcp_pair(u0 - 2)
+                if g_cols(n) > 0:
+                    quad_second(n, True)
             if is_cubic(dx_q(n)):
+                dx_term(dx_q(n), 0)
                 dx_term(dx_q(n), 1)
+            if n >= first_dcp:
+                dcp_advance(2 if 13 < n else 0, nc.vector.tensor_copy)
+            if is_cubic(n - 2) and n < NQ + 2:
+                make_tilt(n - 2)
             if is_quad(n + 1):
                 square(n + 1, 0)
             if is_cubic(n - 3):
-                basis_round(n - 3)
+                basis_round(n - 3, ())
             if is_cubic(dx_q(n)):
                 dx_flip(dx_q(n), 0)
                 dx_flip(dx_q(n), 1)
-            if is_cubic(dx_q(n + 1)):
+            if n == LAG + NK - 1:
+                dx_store(0)
+                p_matmuls(NQ)
+            elif is_cubic(dx_q(n + 1)):
                 p_matmuls(dx_q(n + 1))
-            if is_cubic(n - 2):
-                make_slope(n - 2)
+            if is_quad(n):
+                quad_second(n, False)
             if is_quad(n + 2):
                 clamp(n + 2)
-            if is_quad(n):
-                quad_second(n)
-            dcp_pair(u0)
+            if is_cubic(n - 2) and n >= NQ + 2:
+                make_tilt(n - 2)
+            if n >= first_dcp:
+                dcp_advance(2, nc.scalar.copy)
             if is_quad(n + 1):
                 square(n + 1, 1)
                 square(n + 1, 2)
             quantise_pending()
-            if is_cubic(n - 2):
-                make_tilt(n - 2)
-            if is_cubic(n - 3) and (n - 3) % NQ == 7:
-                basis_quantise(0, 8)
-            if n - 3 == NK - 1:
-                basis_quantise(8, 2)
+            if n == LAG + NK - 1:
+                for g in range(2):
+                    dx_term(NQ, g)
+                for g in range(2):
+                    dx_flip(NQ, g)
+                p_matmuls(NQ + 1)
+            if n in (10, 11):
+                basis_quantise(0, 0, 8, (n - 10,))
+            if n == 21:
+                basis_quantise(1, 0, 8, (0, 1))
+            if n == 12:
+                basis_quantise(0, 0, 8, (2, 3))
+                basis_quantise(0, 8, 2)
             if n < 2:
-                make_g_feat(0, n, "out", n in GF_ON_V)
-                make_g_feat(1, n, "p", n in GF_ON_V)
-            if 1 <= n < 7:
-                make_cp(0, (n - 1) % 2, (n - 1) // 2)
-            if n in (5, 6):
-                load_cp(1, n - 5)
-            if 7 <= n < 13:
-                make_cp(1, (n - 7) % 2, (n - 7) // 2)
-            if 4 <= n < 8:
-                make_g_tok((n - 4) // 2, n % 2)
-        basis_sum(last_basis - 3)
-        basis_round(last_basis - 3)
-        q = dx_q(last_basis)
-        dx_term(q, 0)
-        dx_term(q, 1)
-        dx_flip(q, 0)
-        dx_flip(q, 1)
-        p_matmuls(q + 1)
-        basis_quantise(8, 2)
+                make_g_feat(0, n, "dx", True)
+                make_g_feat(1, n, "p", True)
+            if n in (1, 2):
+                make_cp(2 * n - 2)
+                make_cp(2 * n - 1)
+            for i in ([n + 1] if 3 <= n < 11 else [2 * n - 10, 2 * n - 9] if 11 <= n < 13 else [n + 3] if 13 <= n < 17 else []):
+                make_cp(i)
+            if 2 <= n < 2 + 8:
+                make_g_tok((n - 2) // 4, (n - 2) % 4)
+        last = 2 * NQ - 2
+        basis_sum(last - 1)
+        make_slope(last)
+        basis_round(last - 1)
+        basis_quantise(1, 0, 8, (2,))
+        make_tilt(last)
+        basis_quantise(1, 0, 8, (3,))
+        basis_sum(last)
+        dx_term(last - 1, 0)
+        dx_term(last - 1, 1)
+        basis_round(last, (1,))
+        basis_quantise(1, 8, 2)
+        p_matmuls(last)
         tags = ("out", "out", "basis", "basis")
         for u in range(NCHUNK):
             dcp_matmuls(1, u, tags[u])
         for u in range(units):
             ot, c = divmod(u, NCHUNK)
             dcp_copy(1, u, nc.scalar.copy if u % 2 == 0 else nc.vector.tensor_copy)
+            if u == 0:
+                dx_flip(last - 1, 0)
+                dx_flip(last - 1, 1)
             if u + NCHUNK < units:
                 dcp_matmuls(1, u + NCHUNK, tags[c])
             if u in (1, 3):
-                dx_term(q + 1, u // 2)
+                dx_term(last, u // 2)
             if u == 5:
-                dx_flip(q + 1, 0)
-                dx_flip(q + 1, 1)
-            if u == 7:
+                dx_flip(last, 0)
+                dx_flip(last, 1)
+            if u == 8:
                 dx_store(1)

@@ -24,10 +24,11 @@ JC = 32
 NCHUNK = P // JC
 KGROUPS = ((0, 4), (4, 4), (8, 2))
 LAG = 5
+EXACT = 2
 CP_ON_V = ()
 GF_ON_V = (0, 1)
 DCP_ON_V = (0, 1, 4, 5)
-G_COLS = 832
+G_COLS = 768
 
 
 def tile_kanlayer_v_kernel(tc, x, knots, control_points, grad_out, out_0, out_1):
@@ -67,14 +68,14 @@ def tile_kanlayer_v_kernel(tc, x, knots, control_points, grad_out, out_0, out_1)
             tl = keep.tile([P, n], F32, name=name)
             return tl
 
-        def tt(name, a, b, op):
+        def tt(name, a, b, op, engine=nc.vector):
             o = small(name, a.shape[1])
-            nc.vector.tensor_tensor(out=o[:], in0=a, in1=b, op=op)
+            engine.tensor_tensor(out=o[:], in0=a, in1=b, op=op)
             return o
 
-        def scaled(name, a, c):
+        def scaled(name, a, c, engine=nc.vector):
             o = small(name, a.shape[1])
-            nc.vector.tensor_scalar(out=o[:], in0=a, scalar1=c, scalar2=None, op0=ALU.mult)
+            engine.tensor_scalar(out=o[:], in0=a, scalar1=c, scalar2=None, op0=ALU.mult)
             return o
 
         def recip(name, a):
@@ -82,6 +83,8 @@ def tile_kanlayer_v_kernel(tc, x, knots, control_points, grad_out, out_0, out_1)
             nc.vector.reciprocal(out=o[:], in_=a)
             return o
 
+        residue = small("residue", NQ)
+        nc.gpsimd.memset(residue[:, :EXACT], 0.0)
         ones = small("ones", NK)
         nc.vector.memset(ones[:], 1.0)
         lam = small("lam", NQ)
@@ -91,30 +94,28 @@ def tile_kanlayer_v_kernel(tc, x, knots, control_points, grad_out, out_0, out_1)
         t = small("t", NKNOT)
         nc.vector.tensor_copy(out=t[:], in_=knots_bf[:])
         neg_t = scaled("neg_t", knots_bf[:], -1.0)
-        d1 = tt("d1", t[:, 1:NKNOT], t[:, 0:NKNOT - 1], ALU.subtract)
         d2 = tt("d2", t[:, 2:NKNOT], t[:, 0:NKNOT - 2], ALU.subtract)
+        d1 = tt("d1", t[:, 1:NKNOT], t[:, 0:NKNOT - 1], ALU.subtract)
         d4 = tt("d4", t[:, 4:NKNOT], t[:, 0:NKNOT - 4], ALU.subtract)
         d3 = tt("d3", t[:, 3:NKNOT], t[:, 0:NKNOT - 3], ALU.subtract)
         h_mid = d1[:, 1:NQ + 1]
-        d2d2 = tt("d2d2", d2[:, :NQ], d2[:, 1:], ALU.mult)
-        hh = tt("hh", d1[:, :NQ], d1[:, 2:], ALU.mult)
-        nc.vector.tensor_tensor_scan(out=lam[:, 1:], data0=d4[:], data1=ones[:], initial=1.0, op0=ALU.mult, op1=ALU.mult)
         sig = tt("sig", d2[:, :NQ], d2[:, 1:], ALU.add)
-        prd = tt("prd", d2d2[:], h_mid, ALU.mult)
-        hh2 = tt("hh2", hh[:], hh[:], ALU.mult)
+        inv_d1 = recip("inv_d1", d1[:, EXACT:NQ])
         hd = tt("hd", h_mid, d2[:, 1:], ALU.mult)
-        den = tt("den", prd[:], d3[:], ALU.mult)
-        lam_sig = tt("lam_sig", lam[:], sig[:], ALU.mult)
         inv_sig = recip("inv_sig", sig[:])
-        den2 = tt("den2", den[:], hh2[:], ALU.mult)
-        sig_h = tt("sig_h", sig[:], h_mid, ALU.subtract)
+        d2d2 = tt("d2d2", d2[:, :NQ], d2[:, 1:], ALU.mult)
+        ratio = tt("ratio", d1[:, EXACT + 2:], inv_d1[:], ALU.mult)
+        nc.vector.tensor_tensor_scan(out=lam[:, 1:], data0=d4[:], data1=ones[:], initial=1.0, op0=ALU.mult, op1=ALU.mult)
         peak = tt("peak", hd[:], inv_sig[:], ALU.mult)
-        inv_den = recip("inv_den", den2[:])
-        inv_sig2 = tt("inv_sig2", inv_sig[:], inv_sig[:], ALU.mult)
-        kap_num = tt("kap_num", sig_h[:], prd[:], ALU.mult)
-        gain = tt("gain", lam_sig[:], inv_den[:], ALU.mult)
+        prd = tt("prd", d2d2[:], h_mid, ALU.mult)
+        low = tt("low", t[:, EXACT:NQ], ratio[:], ALU.mult)
+        high = tt("high", t[:, EXACT + 1:NQ + 1], ratio[:], ALU.mult)
         neg_mu = tt("neg_mu", neg_t[:, 1:NQ + 1], peak[:], ALU.subtract)
-        kappa1 = tt("kappa1", kap_num[:], inv_sig2[:], ALU.mult)
+        den = tt("den", prd[:], d3[:], ALU.mult)
+        neg_left = tt("neg_left", t[:, EXACT + 2:NQ + 2], low[:], ALU.subtract)
+        top = tt("top", high[:], t[:, EXACT + 2:NQ + 2], ALU.subtract)
+        plateau = small("plateau", NQ)
+        nc.vector.tensor_tensor(out=plateau[:, :EXACT], in0=d1[:, :EXACT], in1=d1[:, 2:EXACT + 2], op=ALU.mult)
 
         def mx_pair(name, width):
             codes = keep.tile([P, width], U32, name=name + "_codes", align_bytes=64)
@@ -147,8 +148,6 @@ def tile_kanlayer_v_kernel(tc, x, knots, control_points, grad_out, out_0, out_1)
             x_bank.append(bank[:].rearrange("p g t q -> p (g t q)"))
             x_t.append(tl[:])
         nc.scalar.copy(out=x_t[0], in_=x_bank[0])
-        root0 = small("root0", NQ)
-        nc.scalar.activation(out=root0[:], in_=gain[:], func=ACT.Sqrt)
 
         pending = []
 
@@ -170,7 +169,7 @@ def tile_kanlayer_v_kernel(tc, x, knots, control_points, grad_out, out_0, out_1)
                     src = g_raw[g][:, 2 * half + t2, :].bitcast(F32)
                     for u in range(2):
                         nc.tensor.transpose(bank[:, t2, u, :], src[:, 256 * h + u:256 * (h + 1):2], ident[:])
-                copy = nc.vector.tensor_copy if half == 1 else nc.scalar.copy
+                copy = nc.vector.tensor_copy if False else nc.scalar.copy
                 copy(out=words[:, 2 * half:2 * half + 2, :, :], in_=bank[:].rearrange("p t u q -> p t q u"))
             pending.append((st, g_feat[h], g * PASS, PASS, E5M2))
 
@@ -178,7 +177,7 @@ def tile_kanlayer_v_kernel(tc, x, knots, control_points, grad_out, out_0, out_1)
             st = new_stage()
             width = OUT // 4
             src = g_raw[g][:, :, quarter * width:(quarter + 1) * width]
-            copy = nc.vector.tensor_copy if True else nc.scalar.copy
+            copy = nc.vector.tensor_copy if False else nc.scalar.copy
             copy(out=st[:, :PACK * width].rearrange("p (c i t) -> p c t i", i=4, t=PACK),
                                   in_=src.rearrange("p t (c i) -> p c t i", i=4))
             pending.append((st, g_tok[g], quarter * width, width, E5M2))
@@ -199,6 +198,7 @@ def tile_kanlayer_v_kernel(tc, x, knots, control_points, grad_out, out_0, out_1)
             if jh == 0 and k0 + nk == NK:
                 load_cp(1, h)
 
+        ends, mids, falls = {}, {}, {}
         clamped, squares, quad, slope, tilt, p_bank, b_bank, dx_bank = {}, {}, {}, {}, {}, {}, {}, {}
 
         def clamp(q):
@@ -209,34 +209,46 @@ def tile_kanlayer_v_kernel(tc, x, knots, control_points, grad_out, out_0, out_1)
                                         op0=ALU.max, op1=ALU.min)
                 clamped[jh, i] = c
 
-        def square(q, piece):
+        def ramp(q):
             jh, m = divmod(q, NQ)
-            s = work.tile([P, B], F32, name="square", tag=("rise", "mid", "fall")[piece])
-            if piece == 1:
+            z = work.tile([P, B], F32, name="ends", tag="ends")
+            if m >= EXACT:
+                nc.vector.scalar_tensor_tensor(out=z[:], in0=clamped[jh, m][:], scalar=ratio[:, m - EXACT:m - EXACT + 1],
+                                               in1=clamped[jh, m + 2][:], op0=ALU.mult, op1=ALU.subtract)
+            ends[q] = z
+
+        def square_mid(q):
+            jh, m = divmod(q, NQ)
+            s = work.tile([P, B], F32, name="mid", tag="mid")
+            if m >= EXACT:
                 nc.scalar.activation(out=s[:], in_=clamped[jh, m + 1][:], func=ACT.Square,
-                                     bias=mid_bias[:, m:m + 1], scale=root[:, m:m + 1])
+                                     bias=mid_bias[:, m - EXACT:m - EXACT + 1], scale=root[:, m - EXACT:m - EXACT + 1])
             else:
-                knot = m + 3 * (piece // 2)
-                nc.scalar.activation(out=s[:], in_=clamped[jh, m + piece][:], func=ACT.Square, bias=neg_t[:, knot:knot + 1])
-            squares[q, piece] = s
+                nc.scalar.activation(out=s[:], in_=clamped[jh, m + 1][:], func=ACT.Square, bias=neg_mu[:, m:m + 1])
+            mids[q] = s
 
-        def quad_first(q):
+        def square_ends(q):
+            jh, m = divmod(q, NQ)
+            if m >= EXACT:
+                nc.scalar.activation(out=ends[q][:], in_=ends[q][:], func=ACT.Square, bias=neg_left[:, m - EXACT:m - EXACT + 1])
+            else:
+                nc.scalar.activation(out=ends[q][:], in_=clamped[jh, m][:], func=ACT.Square, bias=neg_t[:, m:m + 1])
+                s = work.tile([P, B], F32, name="fall", tag="fall")
+                nc.scalar.activation(out=s[:], in_=clamped[jh, m + 2][:], func=ACT.Square, bias=neg_t[:, m + 3:m + 4])
+                falls[q] = s
+
+        def join_ends(q):
             m = q % NQ
-            rise, mid, fall = squares[q, 0], squares[q, 1], squares.get((q, 2))
-            nc.vector.scalar_tensor_tensor(out=mid[:], in0=mid[:], scalar=kappa[:, m:m + 1], in1=rise[:],
+            nc.vector.scalar_tensor_tensor(out=ends[q][:], in0=ends[q][:], scalar=gain[:, m:m + 1], in1=falls[q][:],
+                                           op0=ALU.mult, op1=ALU.mult)
+
+        def make_quad(q):
+            m = q % NQ
+            top_value = kappa_gain[:, m - EXACT:m - EXACT + 1] if m >= EXACT else kappa[:, m:m + 1]
+            w = work.tile([P, B], F32, name="quad", tag="quad", bufs=3)
+            nc.vector.scalar_tensor_tensor(out=w[:], in0=mids[q][:], scalar=top_value, in1=ends[q][:],
                                            op0=ALU.subtract, op1=ALU.mult)
-
-        def g_cols(q):
-            return 0 if q < 2 else (384 if q < LAG or q in (12, 13) else G_COLS)
-
-        def quad_second(q, on_gpsimd):
-            engine = nc.gpsimd if on_gpsimd else nc.vector
-            mid, fall = squares[q, 1], squares[q, 2]
-            if on_gpsimd or g_cols(q) == 0:
-                w = work.tile([P, B], F32, name="quad", tag="quad", bufs=3)
-                quad[q] = w
-            cols = slice(0, g_cols(q)) if on_gpsimd else slice(g_cols(q), B)
-            engine.tensor_tensor(out=quad[q][:, cols], in0=mid[:, cols], in1=fall[:, cols], op=ALU.mult)
+            quad[q] = w
 
         def make_slope(q):
             k = q % NQ
@@ -248,7 +260,7 @@ def tile_kanlayer_v_kernel(tc, x, knots, control_points, grad_out, out_0, out_1)
         def make_tilt(q):
             jh, k = divmod(q, NQ)
             s = work.tile([P, B], F32, name="tilt", tag="tilt")
-            nc.vector.scalar_tensor_tensor(out=s[:], in0=(x_bank[0], x_t[1])[jh], scalar=t[:, k:k + 1], in1=slope[q][:],
+            nc.vector.scalar_tensor_tensor(out=s[:], in0=x_t[jh], scalar=t[:, k:k + 1], in1=slope[q][:],
                                            op0=ALU.subtract, op1=ALU.mult)
             tilt[q] = s
 
@@ -261,18 +273,12 @@ def tile_kanlayer_v_kernel(tc, x, knots, control_points, grad_out, out_0, out_1)
                     nc.tensor.matmul(bank[:, tk, :], lhsT=tilt[q][:, cols], rhs=ident[:], is_transpose=True, start=False, stop=True)
                 b_bank[q, g] = bank
 
-        def basis_round(q, on_vector=()):
+        def basis_round(q):
             k = q % NQ
-            for g in on_vector:
-                nc.vector.tensor_scalar(out=basis_bf[g][:, :, k, :, :],
-                                        in0=b_bank[q, g][:].rearrange("p t (c j) -> p c j t", c=NCHUNK),
-                                        scalar1=basis_scale[:, k:k + 1], scalar2=None, op0=ALU.mult)
             for g in range(2):
-                if g in on_vector:
-                    continue
                 nc.scalar.activation(out=basis_bf[g][:, :, k, :, :],
                                      in_=b_bank[q, g][:].rearrange("p t (c j) -> p c j t", c=NCHUNK),
-                                     func=ACT.Copy, scale=basis_scale[:, k:k + 1])
+                                     func=ACT.Relu, scale=basis_scale[:, k:k + 1], bias=neg_floor[:, k:k + 1])
 
         def basis_quantise(jh, k0, nk, chunks=range(NCHUNK)):
             for c in chunks:
@@ -370,45 +376,70 @@ def tile_kanlayer_v_kernel(tc, x, knots, control_points, grad_out, out_0, out_1)
                 started.append(v)
 
         clamp(0)
-        square(0, 0)
-        square(0, 2)
-        inv_root0 = recip("inv_root0", root0[:])
-        kappa = tt("kappa", kappa1[:], gain[:], ALU.mult)
+        ramp(0)
+        square_ends(0)
+        square_mid(0)
+        nc.vector.tensor_tensor(out=plateau[:, EXACT:], in0=top[:], in1=neg_left[:], op=ALU.add)
+        lam_sig = tt("lam_sig", lam[:], sig[:], ALU.mult)
+        sig_h = tt("sig_h", sig[:], h_mid, ALU.subtract)
+        plateau2 = tt("plateau2", plateau[:], plateau[:], ALU.mult)
+        inv_sig2 = tt("inv_sig2", inv_sig[:], inv_sig[:], ALU.mult)
+        kap_num = tt("kap_num", sig_h[:], prd[:], ALU.mult)
+        den2 = tt("den2", den[:], plateau2[:], ALU.mult)
+        clamp(1)
+        inv_den = recip("inv_den", den2[:])
+        kappa = tt("kappa", kap_num[:], inv_sig2[:], ALU.mult)
         inv_d4 = recip("inv_d4", d4[:])
-        quot = tt("quot", gain[:], inv_root0[:], ALU.mult)
+        gain = tt("gain", lam_sig[:], inv_den[:], ALU.mult)
         inv_lam = recip("inv_lam", lam[:, :NK])
+        right = tt("right", high[:], t[:, EXACT + 3:NQ + 3], ALU.subtract)
+        root0 = small("root0", NQ - EXACT)
+        nc.scalar.activation(out=root0[:], in_=gain[:, EXACT:], func=ACT.Sqrt)
+        join_ends(0)
         neg_inv_d4 = scaled("neg_inv_d4", inv_d4[:], -1.0)
-        root2 = tt("root2", quot[:], root0[:], ALU.add)
+        gap = tt("gap", right[:], neg_left[:], ALU.add)
+        kappa_gain = tt("kappa_gain", kappa[:, EXACT:], gain[:, EXACT:], ALU.mult)
         basis_scale = scaled("basis_scale", inv_lam[:], -1.0)
         slope_scale = scaled("slope_scale", inv_lam[:], -3.0)
+        inv_root0 = recip("inv_root0", root0[:])
+        gap2 = tt("gap2", gap[:], gap[:], ALU.mult, nc.gpsimd)
+        twice = scaled("twice", inv_lam[:], -2.0, nc.gpsimd)
+        nc.gpsimd.tensor_tensor(out=residue[:, EXACT:], in0=gap2[:], in1=kappa_gain[:], op=ALU.mult)
+        spread = tt("spread", residue[:, 1:], inv_d4[:], ALU.mult, nc.gpsimd)
+        both = tt("both", residue[:, :NK], residue[:, 1:], ALU.add, nc.gpsimd)
+        bound = tt("bound", spread[:], both[:], ALU.add, nc.gpsimd)
+        neg_floor = tt("neg_floor", bound[:], twice[:], ALU.mult, nc.gpsimd)
+        make_quad(0)
+        quot = tt("quot", gain[:, EXACT:], inv_root0[:], ALU.mult)
+        clamp(2)
+        root2 = tt("root2", quot[:], root0[:], ALU.add)
+        half_mu = scaled("half_mu", neg_mu[:, EXACT:], 0.5)
         root = scaled("root", root2[:], 0.5)
-        mid_bias = tt("mid_bias", neg_mu[:], root[:], ALU.mult)
-        square(0, 1)
+        mid_bias = tt("mid_bias", half_mu[:], root2[:], ALU.mult)
         nc.scalar.copy(out=x_t[1], in_=x_bank[1])
-        clamp(1)
         last_basis = 2 * NQ - 2 + 3
         first_dcp = NK + 3
         for n in range(last_basis - 1):
-            u0 = NCHUNK * (n - first_dcp)
             if is_cubic(n - 3):
                 basis_sum(n - 3)
-            if is_cubic(n - 2):
-                make_slope(n - 2)
-            if is_quad(n):
-                quad_first(n)
-                if g_cols(n) > 0:
-                    quad_second(n, True)
+            if is_quad(n + 1):
+                ramp(n + 1)
             if is_cubic(dx_q(n)):
                 dx_term(dx_q(n), 0)
-                dx_term(dx_q(n), 1)
+            if n % NQ < EXACT and n > 0:
+                join_ends(n)
             if n >= first_dcp:
-                dcp_advance(2 if 13 < n else 0, nc.vector.tensor_copy)
-            if is_cubic(n - 2) and n < NQ + 2:
-                make_tilt(n - 2)
+                dcp_advance(2 if 13 < n else 0, nc.scalar.copy)
             if is_quad(n + 1):
-                square(n + 1, 0)
+                square_mid(n + 1)
+            if is_cubic(n - 2):
+                make_slope(n - 2)
+            if is_cubic(dx_q(n)):
+                dx_term(dx_q(n), 1)
+            if n > 0:
+                make_quad(n)
             if is_cubic(n - 3):
-                basis_round(n - 3, ())
+                basis_round(n - 3)
             if is_cubic(dx_q(n)):
                 dx_flip(dx_q(n), 0)
                 dx_flip(dx_q(n), 1)
@@ -417,17 +448,14 @@ def tile_kanlayer_v_kernel(tc, x, knots, control_points, grad_out, out_0, out_1)
                 p_matmuls(NQ)
             elif is_cubic(dx_q(n + 1)):
                 p_matmuls(dx_q(n + 1))
-            if is_quad(n):
-                quad_second(n, False)
-            if is_quad(n + 2):
+            if is_quad(n + 2) and n > 0:
                 clamp(n + 2)
-            if is_cubic(n - 2) and n >= NQ + 2:
+            if is_cubic(n - 2):
                 make_tilt(n - 2)
             if n >= first_dcp:
                 dcp_advance(2, nc.scalar.copy)
             if is_quad(n + 1):
-                square(n + 1, 1)
-                square(n + 1, 2)
+                square_ends(n + 1)
             quantise_pending()
             if n == LAG + NK - 1:
                 for g in range(2):
@@ -450,8 +478,8 @@ def tile_kanlayer_v_kernel(tc, x, knots, control_points, grad_out, out_0, out_1)
                 make_cp(2 * n - 1)
             for i in ([n + 1] if 3 <= n < 11 else [2 * n - 10, 2 * n - 9] if 11 <= n < 13 else [n + 3] if 13 <= n < 17 else []):
                 make_cp(i)
-            if 2 <= n < 2 + 8:
-                make_g_tok((n - 2) // 4, (n - 2) % 4)
+            if 4 <= n < 4 + 8:
+                make_g_tok((n - 4) // 4, (n - 4) % 4)
         last = 2 * NQ - 2
         basis_sum(last - 1)
         make_slope(last)
@@ -462,7 +490,7 @@ def tile_kanlayer_v_kernel(tc, x, knots, control_points, grad_out, out_0, out_1)
         basis_sum(last)
         dx_term(last - 1, 0)
         dx_term(last - 1, 1)
-        basis_round(last, (1,))
+        basis_round(last)
         basis_quantise(1, 8, 2)
         p_matmuls(last)
         tags = ("out", "out", "basis", "basis")

@@ -177,7 +177,7 @@ def tile_kanlayer_v_kernel(tc, x, knots, control_points, grad_out, out_0, out_1)
             st = new_stage()
             width = OUT // 4
             src = g_raw[g][:, :, quarter * width:(quarter + 1) * width]
-            copy = nc.vector.tensor_copy if False else nc.scalar.copy
+            copy = nc.vector.tensor_copy if quarter % 2 == 0 else nc.scalar.copy
             copy(out=st[:, :PACK * width].rearrange("p (c i t) -> p c t i", i=4, t=PACK),
                                   in_=src.rearrange("p t (c i) -> p c t i", i=4))
             pending.append((st, g_tok[g], quarter * width, width, E5M2))
@@ -191,7 +191,8 @@ def tile_kanlayer_v_kernel(tc, x, knots, control_points, grad_out, out_0, out_1)
             if j0 == 0:
                 cp_stage[jh, h, k0] = new_stage()
             st = cp_stage[jh, h, k0]
-            nc.scalar.copy(out=st[:, :nk * PASS].rearrange("p (k j t) -> p j t k", k=nk, t=PACK)[:, j0:j0 + nj, :, :],
+            copy = nc.vector.tensor_copy if False else nc.scalar.copy
+            copy(out=st[:, :nk * PASS].rearrange("p (k j t) -> p j t k", k=nk, t=PACK)[:, j0:j0 + nj, :, :],
                            in_=cp_raw[jh, h][:, :, j0:j0 + nj, k0:k0 + nk].rearrange("p t j k -> p j t k"))
             if j0 + nj == P:
                 pending.append((st, cp_mx[jh, h], k0 * P, nk * P, E4M3))
@@ -233,7 +234,7 @@ def tile_kanlayer_v_kernel(tc, x, knots, control_points, grad_out, out_0, out_1)
                 nc.scalar.activation(out=ends[q][:], in_=ends[q][:], func=ACT.Square, bias=neg_left[:, m - EXACT:m - EXACT + 1])
             else:
                 nc.scalar.activation(out=ends[q][:], in_=clamped[jh, m][:], func=ACT.Square, bias=neg_t[:, m:m + 1])
-                s = work.tile([P, B], F32, name="fall", tag="fall")
+                s = work.tile([P, B], F32, name="fall", tag="fall", bufs=1)
                 nc.scalar.activation(out=s[:], in_=clamped[jh, m + 2][:], func=ACT.Square, bias=neg_t[:, m + 3:m + 4])
                 falls[q] = s
 
@@ -288,10 +289,10 @@ def tile_kanlayer_v_kernel(tc, x, knots, control_points, grad_out, out_0, out_1)
                     nc.vector.quantize_mx(out=codes[:, cols].bitcast(E4M3), scales=scales[:, cols],
                                           in_=basis_bf[g][:, c, k0:k0 + nk, :, :].rearrange("p k j t -> p (k j t)"))
 
-        def p_matmuls(q):
+        def p_matmuls(q, tag="p"):
             jh, k = divmod(q, NQ)
             for g in range(2):
-                bank = psum.tile([P, PASS], F32, name="p_bank", tag="p")
+                bank = psum.tile([P, PASS], F32, name="p_bank", tag=tag)
                 for h in range(2):
                     wc, ws = cp_mx[jh, h]
                     gc, gs = g_feat[h]
@@ -304,7 +305,7 @@ def tile_kanlayer_v_kernel(tc, x, knots, control_points, grad_out, out_0, out_1)
 
         def dx_term(q, g):
             jh, k = divmod(q, NQ)
-            prod = work.tile([P, PASS], F32, name="prod", tag="prod", bufs=3)
+            prod = work.tile([P, PASS], F32, name="prod", tag="prod", bufs=4)
             nc.vector.scalar_tensor_tensor(out=prod[:], in0=slope[q][:, g * PASS:(g + 1) * PASS], scalar=slope_scale[:, k:k + 1],
                                            in1=p_bank[q, g][:], op0=ALU.mult, op1=ALU.mult)
             prods[q, g] = prod
@@ -349,8 +350,10 @@ def tile_kanlayer_v_kernel(tc, x, knots, control_points, grad_out, out_0, out_1)
                 dcp_res[jh, ot] = res
             res = dcp_res[jh, ot]
             copy(out=res[:, c * JC:(c + 1) * JC, :], in_=o_bank[jh, u][:, :SLOTS * JC].rearrange("p (k j) -> p j k", j=JC))
-            if c == NCHUNK - 1:
-                nc.sync.dma_start(out=out_1[ot * P:(ot + 1) * P, jh * P:(jh + 1) * P, :], in_=res[:])
+            per_store = 2 if jh == 1 and ot >= 0 else NCHUNK
+            if (c + 1) % per_store == 0:
+                j0, j1 = (c + 1 - per_store) * JC, (c + 1) * JC
+                nc.sync.dma_start(out=out_1[ot * P:(ot + 1) * P, jh * P + j0:jh * P + j1, :], in_=res[:, j0:j1, :])
 
         def dx_q(n):
             i = n - LAG + (n >= LAG + NK)
@@ -478,36 +481,29 @@ def tile_kanlayer_v_kernel(tc, x, knots, control_points, grad_out, out_0, out_1)
                 make_cp(2 * n - 1)
             for i in ([n + 1] if 3 <= n < 11 else [2 * n - 10, 2 * n - 9] if 11 <= n < 13 else [n + 3] if 13 <= n < 17 else []):
                 make_cp(i)
-            if 4 <= n < 4 + 8:
-                make_g_tok((n - 4) // 4, (n - 4) % 4)
+            if 3 <= n < 3 + 8:
+                make_g_tok((n - 3) // 4, (n - 3) % 4)
         last = 2 * NQ - 2
         basis_sum(last - 1)
+        p_matmuls(last, "out")
         make_slope(last)
         basis_round(last - 1)
         basis_quantise(1, 0, 8, (2,))
         make_tilt(last)
-        basis_quantise(1, 0, 8, (3,))
         basis_sum(last)
-        dx_term(last - 1, 0)
-        dx_term(last - 1, 1)
+        basis_quantise(1, 0, 8, (3,))
+        for q in (last - 1, last):
+            for g in range(2):
+                dx_term(q, g)
+                dx_flip(q, g)
         basis_round(last)
         basis_quantise(1, 8, 2)
-        p_matmuls(last)
-        tags = ("out", "out", "basis", "basis")
-        for u in range(NCHUNK):
+        dx_store(1)
+        tags = ("p", "p", "out", "out", "basis", "basis")
+        ahead = len(tags)
+        for u in range(ahead):
             dcp_matmuls(1, u, tags[u])
         for u in range(units):
-            ot, c = divmod(u, NCHUNK)
-            dcp_copy(1, u, nc.scalar.copy if u % 2 == 0 else nc.vector.tensor_copy)
-            if u == 0:
-                dx_flip(last - 1, 0)
-                dx_flip(last - 1, 1)
-            if u + NCHUNK < units:
-                dcp_matmuls(1, u + NCHUNK, tags[c])
-            if u in (1, 3):
-                dx_term(last, u // 2)
-            if u == 5:
-                dx_flip(last, 0)
-                dx_flip(last, 1)
-            if u == 8:
-                dx_store(1)
+            dcp_copy(1, u, nc.vector.tensor_copy if u % 2 == 0 else nc.scalar.copy)
+            if u + ahead < units:
+                dcp_matmuls(1, u + ahead, tags[u % ahead])

@@ -22,13 +22,18 @@ NQ = NK + 1
 NKNOT = SLOTS + 1
 JC = 32
 NCHUNK = P // JC
-KGROUPS = ((0, 4), (4, 4), (8, 2))
-LAG = 5
+EARLY_K = 8
+K_GROUPS = ((0, 4), (4, 4), (8, 2))
+G_PIECES = 4
 EXACT = 2
-CP_ON_V = ()
-GF_ON_V = (0, 1)
-DCP_ON_V = (0, 1, 4, 5)
-G_COLS = 768
+
+SLOPE_LAG = 2
+BASIS_LAG = 3
+FIRST_DX = 5
+DOUBLE_CP = (1, 2, NQ, NQ + 1)
+FIRST_G_TOK = 4
+FIRST_DCP = NK + BASIS_LAG
+CATCH_UP = FIRST_DX + NK - 1
 
 
 def tile_kanlayer_v_kernel(tc, x, knots, control_points, grad_out, out_0, out_1):
@@ -45,16 +50,16 @@ def tile_kanlayer_v_kernel(tc, x, knots, control_points, grad_out, out_0, out_1)
         nc.sync.dma_start(out=x_raw[:], in_=x.rearrange("(g p t) j -> p g t j", g=2, t=PACK))
         g_raw = []
         for g in range(2):
-            tl = work.tile([P, PACK, OUT], BF16, name="g_raw", tag="io", bufs=3)
-            nc.sync.dma_start(out=tl[:], in_=grad_out[g * PASS:(g + 1) * PASS, :].rearrange("(p t) o -> p t o", t=PACK))
-            g_raw.append(tl)
+            rows = work.tile([P, PACK, OUT], BF16, name="g_raw", tag="io", bufs=3)
+            nc.sync.dma_start(out=rows[:], in_=grad_out[g * PASS:(g + 1) * PASS, :].rearrange("(p t) o -> p t o", t=PACK))
+            g_raw.append(rows)
         cp_raw = {}
 
         def load_cp(jh, h):
-            tl = work.tile([P, PACK, P, SLOTS], BF16, name="cp_raw", tag="cp_raw", align_bytes=64)
+            rows = work.tile([P, PACK, P, SLOTS], BF16, name="cp_raw", tag="cp_raw", align_bytes=64)
             src = control_points[h * PASS:(h + 1) * PASS, jh * P:(jh + 1) * P, :]
-            nc.sync.dma_start(out=tl[:], in_=src.rearrange("(p t) j k -> p t j k", t=PACK))
-            cp_raw[jh, h] = tl
+            nc.sync.dma_start(out=rows[:], in_=src.rearrange("(p t) j k -> p t j k", t=PACK))
+            cp_raw[jh, h] = rows
 
         load_cp(0, 0)
         load_cp(0, 1)
@@ -65,23 +70,23 @@ def tile_kanlayer_v_kernel(tc, x, knots, control_points, grad_out, out_0, out_1)
         make_identity(nc, ident[:])
 
         def small(name, n):
-            tl = keep.tile([P, n], F32, name=name)
-            return tl
+            column = keep.tile([P, n], F32, name=name)
+            return column
 
-        def tt(name, a, b, op, engine=nc.vector):
-            o = small(name, a.shape[1])
-            engine.tensor_tensor(out=o[:], in0=a, in1=b, op=op)
-            return o
+        def combine(name, a, b, op, engine=nc.vector):
+            result = small(name, a.shape[1])
+            engine.tensor_tensor(out=result[:], in0=a, in1=b, op=op)
+            return result
 
-        def scaled(name, a, c, engine=nc.vector):
-            o = small(name, a.shape[1])
-            engine.tensor_scalar(out=o[:], in0=a, scalar1=c, scalar2=None, op0=ALU.mult)
-            return o
+        def scaled(name, a, factor, engine=nc.vector):
+            result = small(name, a.shape[1])
+            engine.tensor_scalar(out=result[:], in0=a, scalar1=factor, scalar2=None, op0=ALU.mult)
+            return result
 
         def recip(name, a):
-            o = small(name, a.shape[1])
-            nc.vector.reciprocal(out=o[:], in_=a)
-            return o
+            result = small(name, a.shape[1])
+            nc.vector.reciprocal(out=result[:], in_=a)
+            return result
 
         residue = small("residue", NQ)
         nc.gpsimd.memset(residue[:, :EXACT], 0.0)
@@ -89,31 +94,30 @@ def tile_kanlayer_v_kernel(tc, x, knots, control_points, grad_out, out_0, out_1)
         nc.vector.memset(ones[:], 1.0)
         lam = small("lam", NQ)
         nc.vector.memset(lam[:, 0:1], 1.0)
-        warm = small("warm", 1)
-        nc.scalar.activation(out=warm[:], in_=ones[:, 0:1], func=ACT.Sqrt)
+        neg_t = small("neg_t", NKNOT)
+        nc.scalar.activation(out=neg_t[:], in_=knots_bf[:], func=ACT.Copy, scale=-1.0)
         t = small("t", NKNOT)
         nc.vector.tensor_copy(out=t[:], in_=knots_bf[:])
-        neg_t = scaled("neg_t", knots_bf[:], -1.0)
-        d2 = tt("d2", t[:, 2:NKNOT], t[:, 0:NKNOT - 2], ALU.subtract)
-        d1 = tt("d1", t[:, 1:NKNOT], t[:, 0:NKNOT - 1], ALU.subtract)
-        d4 = tt("d4", t[:, 4:NKNOT], t[:, 0:NKNOT - 4], ALU.subtract)
-        d3 = tt("d3", t[:, 3:NKNOT], t[:, 0:NKNOT - 3], ALU.subtract)
+        d2 = combine("d2", t[:, 2:NKNOT], t[:, 0:NKNOT - 2], ALU.subtract)
+        d1 = combine("d1", t[:, 1:NKNOT], t[:, 0:NKNOT - 1], ALU.subtract)
+        d4 = combine("d4", t[:, 4:NKNOT], t[:, 0:NKNOT - 4], ALU.subtract)
+        d3 = combine("d3", t[:, 3:NKNOT], t[:, 0:NKNOT - 3], ALU.subtract)
         h_mid = d1[:, 1:NQ + 1]
-        sig = tt("sig", d2[:, :NQ], d2[:, 1:], ALU.add)
+        sig = combine("sig", d2[:, :NQ], d2[:, 1:], ALU.add)
         inv_d1 = recip("inv_d1", d1[:, EXACT:NQ])
-        hd = tt("hd", h_mid, d2[:, 1:], ALU.mult)
+        hd = combine("hd", h_mid, d2[:, 1:], ALU.mult)
         inv_sig = recip("inv_sig", sig[:])
-        d2d2 = tt("d2d2", d2[:, :NQ], d2[:, 1:], ALU.mult)
-        ratio = tt("ratio", d1[:, EXACT + 2:], inv_d1[:], ALU.mult)
+        d2d2 = combine("d2d2", d2[:, :NQ], d2[:, 1:], ALU.mult)
+        ratio = combine("ratio", d1[:, EXACT + 2:], inv_d1[:], ALU.mult)
         nc.vector.tensor_tensor_scan(out=lam[:, 1:], data0=d4[:], data1=ones[:], initial=1.0, op0=ALU.mult, op1=ALU.mult)
-        peak = tt("peak", hd[:], inv_sig[:], ALU.mult)
-        prd = tt("prd", d2d2[:], h_mid, ALU.mult)
-        low = tt("low", t[:, EXACT:NQ], ratio[:], ALU.mult)
-        high = tt("high", t[:, EXACT + 1:NQ + 1], ratio[:], ALU.mult)
-        neg_mu = tt("neg_mu", neg_t[:, 1:NQ + 1], peak[:], ALU.subtract)
-        den = tt("den", prd[:], d3[:], ALU.mult)
-        neg_left = tt("neg_left", t[:, EXACT + 2:NQ + 2], low[:], ALU.subtract)
-        top = tt("top", high[:], t[:, EXACT + 2:NQ + 2], ALU.subtract)
+        peak = combine("peak", hd[:], inv_sig[:], ALU.mult)
+        prd = combine("prd", d2d2[:], h_mid, ALU.mult)
+        low = combine("low", t[:, EXACT:NQ], ratio[:], ALU.mult)
+        high = combine("high", t[:, EXACT + 1:NQ + 1], ratio[:], ALU.mult)
+        neg_mu = combine("neg_mu", neg_t[:, 1:NQ + 1], peak[:], ALU.subtract)
+        den = combine("den", prd[:], d3[:], ALU.mult)
+        neg_left = combine("neg_left", t[:, EXACT + 2:NQ + 2], low[:], ALU.subtract)
+        top = combine("top", high[:], t[:, EXACT + 2:NQ + 2], ALU.subtract)
         plateau = small("plateau", NQ)
         nc.vector.tensor_tensor(out=plateau[:, :EXACT], in0=d1[:, :EXACT], in1=d1[:, 2:EXACT + 2], op=ALU.mult)
 
@@ -125,82 +129,77 @@ def tile_kanlayer_v_kernel(tc, x, knots, control_points, grad_out, out_0, out_1)
         g_feat = [mx_pair("g_feat%d" % h, B) for h in range(2)]
         g_tok = [mx_pair("g_tok%d" % g, OUT) for g in range(2)]
         cp_mx = {(jh, h): mx_pair("cp%d%d" % (jh, h), NK * P) for jh in range(2) for h in range(2)}
-        basis_mx = {(0, g): mx_pair("basis%d" % g, NCHUNK * PASS) for g in range(2)}
-
-        def zero_fill(jh, g):
-            codes, scales = basis_mx[0, g]
+        basis_mx = [mx_pair("basis%d" % g, NCHUNK * PASS) for g in range(2)]
+        basis_bf = []
+        for g in range(2):
+            rounded = keep.tile([P, NCHUNK, NK, JC, PACK], BF16, name="basis_bf%d" % g, align_bytes=64)
+            basis_bf.append(rounded)
+            codes, scales = basis_mx[g]
             nc.gpsimd.memset(codes[:].rearrange("p (c w) -> p c w", c=NCHUNK)[:, :, NK * JC:], 0)
             nc.gpsimd.memset(scales[:].bitcast(U32).rearrange("p (c w) -> p c w", c=NCHUNK)[:, :, NK * JC // 4:], 0)
 
-        basis_bf = []
-        for g in range(2):
-            tl = keep.tile([P, NCHUNK, NK, JC, PACK], BF16, name="basis_bf%d" % g, align_bytes=64)
-            basis_bf.append(tl)
-            zero_fill(0, g)
-
         x_t, x_bank = [], []
         for jh in range(2):
-            tl = keep.tile([P, B], BF16, name="x_t%d" % jh)
+            turned = keep.tile([P, B], BF16, name="x_t%d" % jh)
             bank = psum.tile([P, 2, PACK, P], BF16, name="xt_bank", tag=("out", "basis")[jh])
             for g in range(2):
                 for tk in range(PACK):
                     nc.tensor.transpose(bank[:, g, tk, :], x_raw[:, g, tk, jh * P:(jh + 1) * P], ident_bf[:])
             x_bank.append(bank[:].rearrange("p g t q -> p (g t q)"))
-            x_t.append(tl[:])
+            x_t.append(turned[:])
         nc.scalar.copy(out=x_t[0], in_=x_bank[0])
 
         pending = []
 
         def new_stage():
-            st = work.tile([P, PACK * PASS], BF16, name="stage", tag="stage", bufs=3, align_bytes=64)
-            return st
+            stage = work.tile([P, PACK * PASS], BF16, name="stage", tag="stage", bufs=3, align_bytes=64)
+            return stage
 
         def quantise_pending():
-            for st, (codes, scales), c0, n, fmt in pending:
-                nc.vector.quantize_mx(out=codes[:, c0:c0 + n].bitcast(fmt), scales=scales[:, c0:c0 + n], in_=st[:, :PACK * n])
+            for stage, (codes, scales), c0, n, fmt in pending:
+                nc.vector.quantize_mx(out=codes[:, c0:c0 + n].bitcast(fmt), scales=scales[:, c0:c0 + n], in_=stage[:, :PACK * n])
             pending.clear()
 
-        def make_g_feat(h, g, tags, on_vector):
-            st = new_stage()
-            words = st[:].bitcast(F32).rearrange("p (t q u) -> p t q u", t=PACK, u=2)
+        def make_g_feat(h, g, tag):
+            stage = new_stage()
+            words = stage[:].bitcast(F32).rearrange("p (t q u) -> p t q u", t=PACK, u=2)
             for half in range(2):
-                bank = psum.tile([P, 2, 2, P], F32, name="gt_bank", tag=tags)
+                bank = psum.tile([P, 2, 2, P], F32, name="gt_bank", tag=tag)
                 for t2 in range(2):
                     src = g_raw[g][:, 2 * half + t2, :].bitcast(F32)
                     for u in range(2):
-                        nc.tensor.transpose(bank[:, t2, u, :], src[:, 256 * h + u:256 * (h + 1):2], ident[:])
-                copy = nc.vector.tensor_copy if False else nc.scalar.copy
-                copy(out=words[:, 2 * half:2 * half + 2, :, :], in_=bank[:].rearrange("p t u q -> p t q u"))
-            pending.append((st, g_feat[h], g * PASS, PASS, E5M2))
+                        nc.tensor.transpose(bank[:, t2, u, :], src[:, 2 * P * h + u:2 * P * (h + 1):2], ident[:])
+                nc.scalar.copy(out=words[:, 2 * half:2 * half + 2, :, :], in_=bank[:].rearrange("p t u q -> p t q u"))
+            pending.append((stage, g_feat[h], g * PASS, PASS, E5M2))
 
-        def make_g_tok(g, quarter):
-            st = new_stage()
-            width = OUT // 4
-            src = g_raw[g][:, :, quarter * width:(quarter + 1) * width]
-            copy = nc.vector.tensor_copy if quarter % 2 == 0 else nc.scalar.copy
-            copy(out=st[:, :PACK * width].rearrange("p (c i t) -> p c t i", i=4, t=PACK),
-                                  in_=src.rearrange("p t (c i) -> p c t i", i=4))
-            pending.append((st, g_tok[g], quarter * width, width, E5M2))
+        def make_g_tok(i):
+            g, piece = divmod(i, G_PIECES)
+            stage = new_stage()
+            width = OUT // G_PIECES
+            src = g_raw[g][:, :, piece * width:(piece + 1) * width]
+            nc.scalar.copy(out=stage[:, :PACK * width].rearrange("p (c i t) -> p c t i", i=4, t=PACK),
+                           in_=src.rearrange("p t (c i) -> p c t i", i=4))
+            pending.append((stage, g_tok[g], piece * width, width, E5M2))
 
-        cp_units = [(jh, h, k0, nk, j0, nj) for jh in range(2) for k0, nk in KGROUPS for h in range(2)
-                    for nj in [2 * P // nk] for j0 in range(0, P, nj)]
+        cp_copies = [(jh, h, k0, nk, j0, 2 * P // nk) for jh in range(2) for k0, nk in K_GROUPS for h in range(2)
+                     for j0 in range(0, P, 2 * P // nk)]
+        cp_left = list(range(len(cp_copies)))
         cp_stage = {}
 
         def make_cp(i):
-            jh, h, k0, nk, j0, nj = cp_units[i]
+            jh, h, k0, nk, j0, nj = cp_copies[i]
             if j0 == 0:
                 cp_stage[jh, h, k0] = new_stage()
-            st = cp_stage[jh, h, k0]
-            copy = nc.vector.tensor_copy if False else nc.scalar.copy
-            copy(out=st[:, :nk * PASS].rearrange("p (k j t) -> p j t k", k=nk, t=PACK)[:, j0:j0 + nj, :, :],
+            stage = cp_stage[jh, h, k0]
+            nc.scalar.copy(out=stage[:, :nk * PASS].rearrange("p (k j t) -> p j t k", k=nk, t=PACK)[:, j0:j0 + nj, :, :],
                            in_=cp_raw[jh, h][:, :, j0:j0 + nj, k0:k0 + nk].rearrange("p t j k -> p j t k"))
             if j0 + nj == P:
-                pending.append((st, cp_mx[jh, h], k0 * P, nk * P, E4M3))
+                pending.append((stage, cp_mx[jh, h], k0 * P, nk * P, E4M3))
             if jh == 0 and k0 + nk == NK:
                 load_cp(1, h)
 
-        ends, mids, falls = {}, {}, {}
-        clamped, squares, quad, slope, tilt, p_bank, b_bank, dx_bank = {}, {}, {}, {}, {}, {}, {}, {}
+        clamped, ends, mids, falls, quad, diff, tilt, prods = {}, {}, {}, {}, {}, {}, {}, {}
+        p_bank, b_bank, dx_bank, o_bank, dcp_res = {}, {}, {}, {}, {}
 
         def clamp(q):
             jh, m = divmod(q, NQ)
@@ -220,13 +219,13 @@ def tile_kanlayer_v_kernel(tc, x, knots, control_points, grad_out, out_0, out_1)
 
         def square_mid(q):
             jh, m = divmod(q, NQ)
-            s = work.tile([P, B], F32, name="mid", tag="mid")
+            mid = work.tile([P, B], F32, name="mid", tag="mid")
             if m >= EXACT:
-                nc.scalar.activation(out=s[:], in_=clamped[jh, m + 1][:], func=ACT.Square,
+                nc.scalar.activation(out=mid[:], in_=clamped[jh, m + 1][:], func=ACT.Square,
                                      bias=mid_bias[:, m - EXACT:m - EXACT + 1], scale=root[:, m - EXACT:m - EXACT + 1])
             else:
-                nc.scalar.activation(out=s[:], in_=clamped[jh, m + 1][:], func=ACT.Square, bias=neg_mu[:, m:m + 1])
-            mids[q] = s
+                nc.scalar.activation(out=mid[:], in_=clamped[jh, m + 1][:], func=ACT.Square, bias=neg_mu[:, m:m + 1])
+            mids[q] = mid
 
         def square_ends(q):
             jh, m = divmod(q, NQ)
@@ -234,9 +233,9 @@ def tile_kanlayer_v_kernel(tc, x, knots, control_points, grad_out, out_0, out_1)
                 nc.scalar.activation(out=ends[q][:], in_=ends[q][:], func=ACT.Square, bias=neg_left[:, m - EXACT:m - EXACT + 1])
             else:
                 nc.scalar.activation(out=ends[q][:], in_=clamped[jh, m][:], func=ACT.Square, bias=neg_t[:, m:m + 1])
-                s = work.tile([P, B], F32, name="fall", tag="fall", bufs=1)
-                nc.scalar.activation(out=s[:], in_=clamped[jh, m + 2][:], func=ACT.Square, bias=neg_t[:, m + 3:m + 4])
-                falls[q] = s
+                fall = work.tile([P, B], F32, name="fall", tag="fall", bufs=1)
+                nc.scalar.activation(out=fall[:], in_=clamped[jh, m + 2][:], func=ACT.Square, bias=neg_t[:, m + 3:m + 4])
+                falls[q] = fall
 
         def join_ends(q):
             m = q % NQ
@@ -245,25 +244,25 @@ def tile_kanlayer_v_kernel(tc, x, knots, control_points, grad_out, out_0, out_1)
 
         def make_quad(q):
             m = q % NQ
-            top_value = kappa_gain[:, m - EXACT:m - EXACT + 1] if m >= EXACT else kappa[:, m:m + 1]
+            height = kappa_gain[:, m - EXACT:m - EXACT + 1] if m >= EXACT else kappa[:, m:m + 1]
             w = work.tile([P, B], F32, name="quad", tag="quad", bufs=3)
-            nc.vector.scalar_tensor_tensor(out=w[:], in0=mids[q][:], scalar=top_value, in1=ends[q][:],
+            nc.vector.scalar_tensor_tensor(out=w[:], in0=mids[q][:], scalar=height, in1=ends[q][:],
                                            op0=ALU.subtract, op1=ALU.mult)
             quad[q] = w
 
-        def make_slope(q):
+        def make_diff(q):
             k = q % NQ
-            s = work.tile([P, B], F32, name="slope", tag="slope", bufs=4)
-            nc.vector.scalar_tensor_tensor(out=s[:], in0=quad[q + 1][:], scalar=neg_inv_d4[:, k:k + 1], in1=quad[q][:],
+            d = work.tile([P, B], F32, name="diff", tag="diff", bufs=4)
+            nc.vector.scalar_tensor_tensor(out=d[:], in0=quad[q + 1][:], scalar=neg_inv_d4[:, k:k + 1], in1=quad[q][:],
                                            op0=ALU.mult, op1=ALU.add)
-            slope[q] = s
+            diff[q] = d
 
         def make_tilt(q):
             jh, k = divmod(q, NQ)
-            s = work.tile([P, B], F32, name="tilt", tag="tilt")
-            nc.vector.scalar_tensor_tensor(out=s[:], in0=x_t[jh], scalar=t[:, k:k + 1], in1=slope[q][:],
+            product = work.tile([P, B], F32, name="tilt", tag="tilt")
+            nc.vector.scalar_tensor_tensor(out=product[:], in0=x_t[jh], scalar=t[:, k:k + 1], in1=diff[q][:],
                                            op0=ALU.subtract, op1=ALU.mult)
-            tilt[q] = s
+            tilt[q] = product
 
         def basis_sum(q):
             for g in range(2):
@@ -281,13 +280,13 @@ def tile_kanlayer_v_kernel(tc, x, knots, control_points, grad_out, out_0, out_1)
                                      in_=b_bank[q, g][:].rearrange("p t (c j) -> p c j t", c=NCHUNK),
                                      func=ACT.Relu, scale=basis_scale[:, k:k + 1], bias=neg_floor[:, k:k + 1])
 
-        def basis_quantise(jh, k0, nk, chunks=range(NCHUNK)):
+        def basis_quantise(k0, k1, chunks):
             for c in chunks:
                 for g in range(2):
-                    codes, scales = basis_mx[0, g]
-                    cols = slice(c * PASS + k0 * JC, c * PASS + (k0 + nk) * JC)
+                    codes, scales = basis_mx[g]
+                    cols = slice(c * PASS + k0 * JC, c * PASS + k1 * JC)
                     nc.vector.quantize_mx(out=codes[:, cols].bitcast(E4M3), scales=scales[:, cols],
-                                          in_=basis_bf[g][:, c, k0:k0 + nk, :, :].rearrange("p k j t -> p (k j t)"))
+                                          in_=basis_bf[g][:, c, k0:k1, :, :].rearrange("p k j t -> p (k j t)"))
 
         def p_matmuls(q, tag="p"):
             jh, k = divmod(q, NQ)
@@ -301,23 +300,20 @@ def tile_kanlayer_v_kernel(tc, x, knots, control_points, grad_out, out_0, out_1)
                                         start=(h == 0), stop=(h == 1))
                 p_bank[q, g] = bank
 
-        prods = {}
-
         def dx_term(q, g):
-            jh, k = divmod(q, NQ)
+            k = q % NQ
             prod = work.tile([P, PASS], F32, name="prod", tag="prod", bufs=4)
-            nc.vector.scalar_tensor_tensor(out=prod[:], in0=slope[q][:, g * PASS:(g + 1) * PASS], scalar=slope_scale[:, k:k + 1],
+            nc.vector.scalar_tensor_tensor(out=prod[:], in0=diff[q][:, g * PASS:(g + 1) * PASS], scalar=slope_scale[:, k:k + 1],
                                            in1=p_bank[q, g][:], op0=ALU.mult, op1=ALU.mult)
             prods[q, g] = prod
 
-        def dx_flip(q, g):
+        def dx_add(q, g):
             jh, k = divmod(q, NQ)
-            prod = prods[q, g]
             if k == 0:
                 bank = psum.tile([P, PACK, P], F32, name="dx_bank", tag="dx")
                 dx_bank[jh, g] = bank
             for tk in range(PACK):
-                nc.tensor.matmul(dx_bank[jh, g][:, tk, :], lhsT=prod[:, tk * P:(tk + 1) * P], rhs=ident[:], is_transpose=True,
+                nc.tensor.matmul(dx_bank[jh, g][:, tk, :], lhsT=prods[q, g][:, tk * P:(tk + 1) * P], rhs=ident[:], is_transpose=True,
                                  start=(k == 0 and tk == 0), stop=(k == NK - 1 and tk == PACK - 1))
 
         def dx_store(jh):
@@ -327,14 +323,14 @@ def tile_kanlayer_v_kernel(tc, x, knots, control_points, grad_out, out_0, out_1)
                 dst = out_0[g * PASS:(g + 1) * PASS, jh * P:(jh + 1) * P]
                 nc.sync.dma_start(out=dst.rearrange("(p t) j -> p t j", t=PACK), in_=res[:])
 
-        dcp_res, o_bank = {}, {}
+        n_banks = OUT // P * NCHUNK
 
         def dcp_matmuls(jh, u, tag):
             ot, c = divmod(u, NCHUNK)
             bank = psum.tile([P, PASS], F32, name="o_bank", tag=tag)
             for g in range(2):
                 gc, gs = g_tok[g]
-                bc, bs = basis_mx[0, g]
+                bc, bs = basis_mx[g]
                 nc.tensor.matmul_mx(out=bank[:], lhsT=gc[:, ot * P:(ot + 1) * P].bitcast(E5M2), lhsT_scale=gs[:, ot * P:(ot + 1) * P],
                                     rhs=bc[:, c * PASS:(c + 1) * PASS].bitcast(E4M3), rhs_scale=bs[:, c * PASS:(c + 1) * PASS],
                                     start=(g == 0), stop=(g == 1))
@@ -350,14 +346,17 @@ def tile_kanlayer_v_kernel(tc, x, knots, control_points, grad_out, out_0, out_1)
                 dcp_res[jh, ot] = res
             res = dcp_res[jh, ot]
             copy(out=res[:, c * JC:(c + 1) * JC, :], in_=o_bank[jh, u][:, :SLOTS * JC].rearrange("p (k j) -> p j k", j=JC))
-            per_store = 2 if jh == 1 and ot >= 0 else NCHUNK
+            per_store = (NCHUNK, NCHUNK // 2)[jh]
             if (c + 1) % per_store == 0:
                 j0, j1 = (c + 1 - per_store) * JC, (c + 1) * JC
                 nc.sync.dma_start(out=out_1[ot * P:(ot + 1) * P, jh * P + j0:jh * P + j1, :], in_=res[:, j0:j1, :])
 
-        def dx_q(n):
-            i = n - LAG + (n >= LAG + NK)
-            return i + i // NK if 0 <= i < 2 * NK else -1
+        def dcp_pair(u):
+            for v in (u, u + 1):
+                if 0 <= v - 2 < n_banks:
+                    dcp_copy(0, v - 2, nc.scalar.copy)
+                if 0 <= v < n_banks:
+                    dcp_matmuls(0, v, "out")
 
         def is_quad(q):
             return 0 <= q < 2 * NQ
@@ -365,145 +364,135 @@ def tile_kanlayer_v_kernel(tc, x, knots, control_points, grad_out, out_0, out_1)
         def is_cubic(q):
             return is_quad(q) and q % NQ < NK
 
-        units = OUT // P * NCHUNK
-
-        started = []
-
-        def dcp_advance(count, copy):
-            for v in range(count):
-                done = len(started) - 2
-                if 0 <= done < units:
-                    dcp_copy(0, done, copy)
-                if len(started) < units:
-                    dcp_matmuls(0, len(started), "out")
-                started.append(v)
+        def dx_of_step(n):
+            i = n - FIRST_DX + (n > CATCH_UP)
+            return i + i // NK if 0 <= i < 2 * NK else -1
 
         clamp(0)
         ramp(0)
         square_ends(0)
         square_mid(0)
         nc.vector.tensor_tensor(out=plateau[:, EXACT:], in0=top[:], in1=neg_left[:], op=ALU.add)
-        lam_sig = tt("lam_sig", lam[:], sig[:], ALU.mult)
-        sig_h = tt("sig_h", sig[:], h_mid, ALU.subtract)
-        plateau2 = tt("plateau2", plateau[:], plateau[:], ALU.mult)
-        inv_sig2 = tt("inv_sig2", inv_sig[:], inv_sig[:], ALU.mult)
-        kap_num = tt("kap_num", sig_h[:], prd[:], ALU.mult)
-        den2 = tt("den2", den[:], plateau2[:], ALU.mult)
+        lam_sig = combine("lam_sig", lam[:], sig[:], ALU.mult)
+        sig_h = combine("sig_h", sig[:], h_mid, ALU.subtract)
+        plateau2 = combine("plateau2", plateau[:], plateau[:], ALU.mult)
+        inv_sig2 = combine("inv_sig2", inv_sig[:], inv_sig[:], ALU.mult)
+        kap_num = combine("kap_num", sig_h[:], prd[:], ALU.mult)
+        den2 = combine("den2", den[:], plateau2[:], ALU.mult)
         clamp(1)
         inv_den = recip("inv_den", den2[:])
-        kappa = tt("kappa", kap_num[:], inv_sig2[:], ALU.mult)
+        kappa = combine("kappa", kap_num[:], inv_sig2[:], ALU.mult)
         inv_d4 = recip("inv_d4", d4[:])
-        gain = tt("gain", lam_sig[:], inv_den[:], ALU.mult)
+        gain = combine("gain", lam_sig[:], inv_den[:], ALU.mult)
         inv_lam = recip("inv_lam", lam[:, :NK])
-        right = tt("right", high[:], t[:, EXACT + 3:NQ + 3], ALU.subtract)
+        right = combine("right", high[:], t[:, EXACT + 3:NQ + 3], ALU.subtract)
         root0 = small("root0", NQ - EXACT)
         nc.scalar.activation(out=root0[:], in_=gain[:, EXACT:], func=ACT.Sqrt)
         join_ends(0)
         neg_inv_d4 = scaled("neg_inv_d4", inv_d4[:], -1.0)
-        gap = tt("gap", right[:], neg_left[:], ALU.add)
-        kappa_gain = tt("kappa_gain", kappa[:, EXACT:], gain[:, EXACT:], ALU.mult)
+        gap = combine("gap", right[:], neg_left[:], ALU.add)
+        kappa_gain = combine("kappa_gain", kappa[:, EXACT:], gain[:, EXACT:], ALU.mult)
         basis_scale = scaled("basis_scale", inv_lam[:], -1.0)
         slope_scale = scaled("slope_scale", inv_lam[:], -3.0)
         inv_root0 = recip("inv_root0", root0[:])
-        gap2 = tt("gap2", gap[:], gap[:], ALU.mult, nc.gpsimd)
+        gap2 = combine("gap2", gap[:], gap[:], ALU.mult, nc.gpsimd)
         twice = scaled("twice", inv_lam[:], -2.0, nc.gpsimd)
         nc.gpsimd.tensor_tensor(out=residue[:, EXACT:], in0=gap2[:], in1=kappa_gain[:], op=ALU.mult)
-        spread = tt("spread", residue[:, 1:], inv_d4[:], ALU.mult, nc.gpsimd)
-        both = tt("both", residue[:, :NK], residue[:, 1:], ALU.add, nc.gpsimd)
-        bound = tt("bound", spread[:], both[:], ALU.add, nc.gpsimd)
-        neg_floor = tt("neg_floor", bound[:], twice[:], ALU.mult, nc.gpsimd)
+        spread = combine("spread", residue[:, 1:], inv_d4[:], ALU.mult, nc.gpsimd)
+        both = combine("both", residue[:, :NK], residue[:, 1:], ALU.add, nc.gpsimd)
+        bound = combine("bound", spread[:], both[:], ALU.add, nc.gpsimd)
+        neg_floor = combine("neg_floor", bound[:], twice[:], ALU.mult, nc.gpsimd)
         make_quad(0)
-        quot = tt("quot", gain[:, EXACT:], inv_root0[:], ALU.mult)
+        quot = combine("quot", gain[:, EXACT:], inv_root0[:], ALU.mult)
         clamp(2)
-        root2 = tt("root2", quot[:], root0[:], ALU.add)
+        root2 = combine("root2", quot[:], root0[:], ALU.add)
         half_mu = scaled("half_mu", neg_mu[:, EXACT:], 0.5)
         root = scaled("root", root2[:], 0.5)
-        mid_bias = tt("mid_bias", half_mu[:], root2[:], ALU.mult)
+        mid_bias = combine("mid_bias", half_mu[:], root2[:], ALU.mult)
         nc.scalar.copy(out=x_t[1], in_=x_bank[1])
-        last_basis = 2 * NQ - 2 + 3
-        first_dcp = NK + 3
-        for n in range(last_basis - 1):
-            if is_cubic(n - 3):
-                basis_sum(n - 3)
+
+        for n in range(2 * NQ):
+            dx_q = dx_of_step(n)
+            u0 = NCHUNK * (n - FIRST_DCP)
+            if is_cubic(n - BASIS_LAG):
+                basis_sum(n - BASIS_LAG)
             if is_quad(n + 1):
                 ramp(n + 1)
-            if is_cubic(dx_q(n)):
-                dx_term(dx_q(n), 0)
+            if is_cubic(dx_q):
+                dx_term(dx_q, 0)
             if n % NQ < EXACT and n > 0:
                 join_ends(n)
-            if n >= first_dcp:
-                dcp_advance(2 if 13 < n else 0, nc.scalar.copy)
+            dcp_pair(u0 - 2)
             if is_quad(n + 1):
                 square_mid(n + 1)
-            if is_cubic(n - 2):
-                make_slope(n - 2)
-            if is_cubic(dx_q(n)):
-                dx_term(dx_q(n), 1)
+            if is_cubic(n - SLOPE_LAG):
+                make_diff(n - SLOPE_LAG)
+            if is_cubic(dx_q):
+                dx_term(dx_q, 1)
             if n > 0:
                 make_quad(n)
-            if is_cubic(n - 3):
-                basis_round(n - 3)
-            if is_cubic(dx_q(n)):
-                dx_flip(dx_q(n), 0)
-                dx_flip(dx_q(n), 1)
-            if n == LAG + NK - 1:
+            if is_cubic(n - BASIS_LAG):
+                basis_round(n - BASIS_LAG)
+            if is_cubic(dx_q):
+                dx_add(dx_q, 0)
+                dx_add(dx_q, 1)
+            if n == CATCH_UP:
                 dx_store(0)
                 p_matmuls(NQ)
-            elif is_cubic(dx_q(n + 1)):
-                p_matmuls(dx_q(n + 1))
+            elif is_cubic(dx_of_step(n + 1)):
+                p_matmuls(dx_of_step(n + 1))
             if is_quad(n + 2) and n > 0:
                 clamp(n + 2)
-            if is_cubic(n - 2):
-                make_tilt(n - 2)
-            if n >= first_dcp:
-                dcp_advance(2, nc.scalar.copy)
+            if is_cubic(n - SLOPE_LAG):
+                make_tilt(n - SLOPE_LAG)
+            dcp_pair(u0)
             if is_quad(n + 1):
                 square_ends(n + 1)
             quantise_pending()
-            if n == LAG + NK - 1:
+            if n == CATCH_UP:
                 for g in range(2):
                     dx_term(NQ, g)
                 for g in range(2):
-                    dx_flip(NQ, g)
+                    dx_add(NQ, g)
                 p_matmuls(NQ + 1)
-            if n in (10, 11):
-                basis_quantise(0, 0, 8, (n - 10,))
-            if n == 21:
-                basis_quantise(1, 0, 8, (0, 1))
-            if n == 12:
-                basis_quantise(0, 0, 8, (2, 3))
-                basis_quantise(0, 8, 2)
+            if n in (FIRST_DCP - 3, FIRST_DCP - 2):
+                basis_quantise(0, EARLY_K, [n - (FIRST_DCP - 3)])
+            if n == FIRST_DCP - 1:
+                basis_quantise(0, EARLY_K, [2, 3])
+                basis_quantise(EARLY_K, NK, range(NCHUNK))
+            if n == 2 * NQ - 1:
+                basis_quantise(0, EARLY_K, [0, 1])
             if n < 2:
-                make_g_feat(0, n, "dx", True)
-                make_g_feat(1, n, "p", True)
-            if n in (1, 2):
-                make_cp(2 * n - 2)
-                make_cp(2 * n - 1)
-            for i in ([n + 1] if 3 <= n < 11 else [2 * n - 10, 2 * n - 9] if 11 <= n < 13 else [n + 3] if 13 <= n < 17 else []):
-                make_cp(i)
-            if 3 <= n < 3 + 8:
-                make_g_tok((n - 3) // 4, (n - 3) % 4)
+                make_g_feat(0, n, "dx")
+                make_g_feat(1, n, "p")
+            if n > 0:
+                for i in cp_left[:2 if n in DOUBLE_CP else 1]:
+                    make_cp(i)
+                    cp_left.remove(i)
+            if 0 <= n - FIRST_G_TOK < 2 * G_PIECES:
+                make_g_tok(n - FIRST_G_TOK)
+
         last = 2 * NQ - 2
         basis_sum(last - 1)
         p_matmuls(last, "out")
-        make_slope(last)
+        make_diff(last)
         basis_round(last - 1)
-        basis_quantise(1, 0, 8, (2,))
+        basis_quantise(0, EARLY_K, [2])
         make_tilt(last)
         basis_sum(last)
-        basis_quantise(1, 0, 8, (3,))
+        basis_quantise(0, EARLY_K, [3])
         for q in (last - 1, last):
             for g in range(2):
                 dx_term(q, g)
-                dx_flip(q, g)
+                dx_add(q, g)
         basis_round(last)
-        basis_quantise(1, 8, 2)
+        basis_quantise(EARLY_K, NK, range(NCHUNK))
         dx_store(1)
+
         tags = ("p", "p", "out", "out", "basis", "basis")
-        ahead = len(tags)
-        for u in range(ahead):
+        for u in range(len(tags)):
             dcp_matmuls(1, u, tags[u])
-        for u in range(units):
+        for u in range(n_banks):
             dcp_copy(1, u, nc.vector.tensor_copy if u % 2 == 0 else nc.scalar.copy)
-            if u + ahead < units:
-                dcp_matmuls(1, u + ahead, tags[u % ahead])
+            if u + len(tags) < n_banks:
+                dcp_matmuls(1, u + len(tags), tags[u % len(tags)])

from contextlib import ExitStack

import concourse.mybir as mybir
from concourse.masks import make_identity

B, IN, OUT, NK, SLOTS = 1024, 256, 1024, 10, 13
FLOPS = 2 * 2 * B * OUT * IN * NK

F32 = mybir.dt.float32
BF16 = mybir.dt.bfloat16
U32 = mybir.dt.uint32
U8 = mybir.dt.uint8
E4M3 = mybir.dt.float8_e4m3fn_x4
E5M2 = mybir.dt.float8_e5m2_x4
ALU = mybir.AluOpType
ACT = mybir.ActivationFunctionType

P = 128
PACK = 4
PASS = P * PACK
NQ = NK + 1
NKNOT = SLOTS + 1
JC = 32
NCHUNK = P // JC
EARLY_K = 8
K_GROUPS = ((0, 4), (4, 4), (8, 2))
G_PIECES = 4
EXACT = 2

SLOPE_LAG = 2
BASIS_LAG = 3
FIRST_DX = 5
DOUBLE_CP = (1, 2, NQ, NQ + 1)
FIRST_G_TOK = 4
FIRST_DCP = NK + BASIS_LAG
CATCH_UP = FIRST_DX + NK - 1


def tile_kanlayer_v_kernel(tc, x, knots, control_points, grad_out, out_0, out_1):
    nc = tc.nc
    with ExitStack() as ctx:
        keep = ctx.enter_context(tc.tile_pool(name="keep", bufs=1))
        work = ctx.enter_context(tc.tile_pool(name="work", bufs=2))
        psum = ctx.enter_context(tc.psum_pool(name="psum", bufs=2))
        ctx.enter_context(tc.manual_schedule())

        knots_bf = keep.tile([P, NKNOT], BF16, name="knots_bf")
        nc.scalar.dma_start(out=knots_bf[:], in_=knots.partition_broadcast(P))
        x_raw = work.tile([P, 2, PACK, IN], BF16, name="x_raw", tag="tilt")
        nc.sync.dma_start(out=x_raw[:], in_=x.rearrange("(g p t) j -> p g t j", g=2, t=PACK))
        g_raw = []
        for g in range(2):
            rows = work.tile([P, PACK, OUT], BF16, name="g_raw", tag="io", bufs=3)
            nc.sync.dma_start(out=rows[:], in_=grad_out[g * PASS:(g + 1) * PASS, :].rearrange("(p t) o -> p t o", t=PACK))
            g_raw.append(rows)
        cp_raw = {}

        def load_cp(jh, h):
            rows = work.tile([P, PACK, P, SLOTS], BF16, name="cp_raw", tag="cp_raw", align_bytes=64)
            src = control_points[h * PASS:(h + 1) * PASS, jh * P:(jh + 1) * P, :]
            nc.sync.dma_start(out=rows[:], in_=src.rearrange("(p t) j k -> p t j k", t=PACK))
            cp_raw[jh, h] = rows

        load_cp(0, 0)
        load_cp(0, 1)

        ident_bf = keep.tile([P, P], BF16, name="ident_bf")
        make_identity(nc, ident_bf[:])
        ident = keep.tile([P, P], F32, name="ident")
        make_identity(nc, ident[:])

        def small(name, n):
            column = keep.tile([P, n], F32, name=name)
            return column

        def combine(name, a, b, op, engine=nc.vector):
            result = small(name, a.shape[1])
            engine.tensor_tensor(out=result[:], in0=a, in1=b, op=op)
            return result

        def scaled(name, a, factor, engine=nc.vector):
            result = small(name, a.shape[1])
            engine.tensor_scalar(out=result[:], in0=a, scalar1=factor, scalar2=None, op0=ALU.mult)
            return result

        def recip(name, a):
            result = small(name, a.shape[1])
            nc.vector.reciprocal(out=result[:], in_=a)
            return result

        residue = small("residue", NQ)
        nc.gpsimd.memset(residue[:, :EXACT], 0.0)
        ones = small("ones", NK)
        nc.vector.memset(ones[:], 1.0)
        lam = small("lam", NQ)
        nc.vector.memset(lam[:, 0:1], 1.0)
        neg_t = small("neg_t", NKNOT)
        nc.scalar.activation(out=neg_t[:], in_=knots_bf[:], func=ACT.Copy, scale=-1.0)
        t = small("t", NKNOT)
        nc.vector.tensor_copy(out=t[:], in_=knots_bf[:])
        d2 = combine("d2", t[:, 2:NKNOT], t[:, 0:NKNOT - 2], ALU.subtract)
        d1 = combine("d1", t[:, 1:NKNOT], t[:, 0:NKNOT - 1], ALU.subtract)
        d4 = combine("d4", t[:, 4:NKNOT], t[:, 0:NKNOT - 4], ALU.subtract)
        d3 = combine("d3", t[:, 3:NKNOT], t[:, 0:NKNOT - 3], ALU.subtract)
        h_mid = d1[:, 1:NQ + 1]
        sig = combine("sig", d2[:, :NQ], d2[:, 1:], ALU.add)
        inv_d1 = recip("inv_d1", d1[:, EXACT:NQ])
        hd = combine("hd", h_mid, d2[:, 1:], ALU.mult)
        inv_sig = recip("inv_sig", sig[:])
        d2d2 = combine("d2d2", d2[:, :NQ], d2[:, 1:], ALU.mult)
        ratio = combine("ratio", d1[:, EXACT + 2:], inv_d1[:], ALU.mult)
        nc.vector.tensor_tensor_scan(out=lam[:, 1:], data0=d4[:], data1=ones[:], initial=1.0, op0=ALU.mult, op1=ALU.mult)
        peak = combine("peak", hd[:], inv_sig[:], ALU.mult)
        prd = combine("prd", d2d2[:], h_mid, ALU.mult)
        low = combine("low", t[:, EXACT:NQ], ratio[:], ALU.mult)
        high = combine("high", t[:, EXACT + 1:NQ + 1], ratio[:], ALU.mult)
        neg_mu = combine("neg_mu", neg_t[:, 1:NQ + 1], peak[:], ALU.subtract)
        den = combine("den", prd[:], d3[:], ALU.mult)
        neg_left = combine("neg_left", t[:, EXACT + 2:NQ + 2], low[:], ALU.subtract)
        top = combine("top", high[:], t[:, EXACT + 2:NQ + 2], ALU.subtract)
        plateau = small("plateau", NQ)
        nc.vector.tensor_tensor(out=plateau[:, :EXACT], in0=d1[:, :EXACT], in1=d1[:, 2:EXACT + 2], op=ALU.mult)

        def mx_pair(name, width):
            codes = keep.tile([P, width], U32, name=name + "_codes", align_bytes=64)
            scales = keep.tile([P, width], U8, name=name + "_scales", align_bytes=64)
            return codes, scales

        g_feat = [mx_pair("g_feat%d" % h, B) for h in range(2)]
        g_tok = [mx_pair("g_tok%d" % g, OUT) for g in range(2)]
        cp_mx = {(jh, h): mx_pair("cp%d%d" % (jh, h), NK * P) for jh in range(2) for h in range(2)}
        basis_mx = [mx_pair("basis%d" % g, NCHUNK * PASS) for g in range(2)]
        basis_bf = []
        for g in range(2):
            rounded = keep.tile([P, NCHUNK, NK, JC, PACK], BF16, name="basis_bf%d" % g, align_bytes=64)
            basis_bf.append(rounded)
            codes, scales = basis_mx[g]
            nc.gpsimd.memset(codes[:].rearrange("p (c w) -> p c w", c=NCHUNK)[:, :, NK * JC:], 0)
            nc.gpsimd.memset(scales[:].bitcast(U32).rearrange("p (c w) -> p c w", c=NCHUNK)[:, :, NK * JC // 4:], 0)

        x_t, x_bank = [], []
        for jh in range(2):
            turned = keep.tile([P, B], BF16, name="x_t%d" % jh)
            bank = psum.tile([P, 2, PACK, P], BF16, name="xt_bank", tag=("out", "basis")[jh])
            for g in range(2):
                for tk in range(PACK):
                    nc.tensor.transpose(bank[:, g, tk, :], x_raw[:, g, tk, jh * P:(jh + 1) * P], ident_bf[:])
            x_bank.append(bank[:].rearrange("p g t q -> p (g t q)"))
            x_t.append(turned[:])
        nc.scalar.copy(out=x_t[0], in_=x_bank[0])

        pending = []

        def new_stage():
            stage = work.tile([P, PACK * PASS], BF16, name="stage", tag="stage", bufs=3, align_bytes=64)
            return stage

        def quantise_pending():
            for stage, (codes, scales), c0, n, fmt in pending:
                nc.vector.quantize_mx(out=codes[:, c0:c0 + n].bitcast(fmt), scales=scales[:, c0:c0 + n], in_=stage[:, :PACK * n])
            pending.clear()

        def make_g_feat(h, g, tag):
            stage = new_stage()
            words = stage[:].bitcast(F32).rearrange("p (t q u) -> p t q u", t=PACK, u=2)
            for half in range(2):
                bank = psum.tile([P, 2, 2, P], F32, name="gt_bank", tag=tag)
                for t2 in range(2):
                    src = g_raw[g][:, 2 * half + t2, :].bitcast(F32)
                    for u in range(2):
                        nc.tensor.transpose(bank[:, t2, u, :], src[:, 2 * P * h + u:2 * P * (h + 1):2], ident[:])
                nc.scalar.copy(out=words[:, 2 * half:2 * half + 2, :, :], in_=bank[:].rearrange("p t u q -> p t q u"))
            pending.append((stage, g_feat[h], g * PASS, PASS, E5M2))

        def make_g_tok(i):
            g, piece = divmod(i, G_PIECES)
            stage = new_stage()
            width = OUT // G_PIECES
            src = g_raw[g][:, :, piece * width:(piece + 1) * width]
            nc.scalar.copy(out=stage[:, :PACK * width].rearrange("p (c i t) -> p c t i", i=4, t=PACK),
                           in_=src.rearrange("p t (c i) -> p c t i", i=4))
            pending.append((stage, g_tok[g], piece * width, width, E5M2))

        cp_copies = [(jh, h, k0, nk, j0, 2 * P // nk) for jh in range(2) for k0, nk in K_GROUPS for h in range(2)
                     for j0 in range(0, P, 2 * P // nk)]
        cp_left = list(range(len(cp_copies)))
        cp_stage = {}

        def make_cp(i):
            jh, h, k0, nk, j0, nj = cp_copies[i]
            if j0 == 0:
                cp_stage[jh, h, k0] = new_stage()
            stage = cp_stage[jh, h, k0]
            nc.scalar.copy(out=stage[:, :nk * PASS].rearrange("p (k j t) -> p j t k", k=nk, t=PACK)[:, j0:j0 + nj, :, :],
                           in_=cp_raw[jh, h][:, :, j0:j0 + nj, k0:k0 + nk].rearrange("p t j k -> p j t k"))
            if j0 + nj == P:
                pending.append((stage, cp_mx[jh, h], k0 * P, nk * P, E4M3))
            if jh == 0 and k0 + nk == NK:
                load_cp(1, h)

        clamped, ends, mids, falls, quad, diff, tilt, prods = {}, {}, {}, {}, {}, {}, {}, {}
        p_bank, b_bank, dx_bank, o_bank, dcp_res = {}, {}, {}, {}, {}

        def clamp(q):
            jh, m = divmod(q, NQ)
            for i in (range(3) if m == 0 else [m + 2]):
                c = work.tile([P, B], BF16, name="clamped", tag="clamped", bufs=5)
                nc.vector.tensor_scalar(out=c[:], in0=x_t[jh], scalar1=t[:, i:i + 1], scalar2=t[:, i + 1:i + 2],
                                        op0=ALU.max, op1=ALU.min)
                clamped[jh, i] = c

        def ramp(q):
            jh, m = divmod(q, NQ)
            z = work.tile([P, B], F32, name="ends", tag="ends")
            if m >= EXACT:
                nc.vector.scalar_tensor_tensor(out=z[:], in0=clamped[jh, m][:], scalar=ratio[:, m - EXACT:m - EXACT + 1],
                                               in1=clamped[jh, m + 2][:], op0=ALU.mult, op1=ALU.subtract)
            ends[q] = z

        def square_mid(q):
            jh, m = divmod(q, NQ)
            mid = work.tile([P, B], F32, name="mid", tag="mid")
            if m >= EXACT:
                nc.scalar.activation(out=mid[:], in_=clamped[jh, m + 1][:], func=ACT.Square,
                                     bias=mid_bias[:, m - EXACT:m - EXACT + 1], scale=root[:, m - EXACT:m - EXACT + 1])
            else:
                nc.scalar.activation(out=mid[:], in_=clamped[jh, m + 1][:], func=ACT.Square, bias=neg_mu[:, m:m + 1])
            mids[q] = mid

        def square_ends(q):
            jh, m = divmod(q, NQ)
            if m >= EXACT:
                nc.scalar.activation(out=ends[q][:], in_=ends[q][:], func=ACT.Square, bias=neg_left[:, m - EXACT:m - EXACT + 1])
            else:
                nc.scalar.activation(out=ends[q][:], in_=clamped[jh, m][:], func=ACT.Square, bias=neg_t[:, m:m + 1])
                fall = work.tile([P, B], F32, name="fall", tag="fall", bufs=1)
                nc.scalar.activation(out=fall[:], in_=clamped[jh, m + 2][:], func=ACT.Square, bias=neg_t[:, m + 3:m + 4])
                falls[q] = fall

        def join_ends(q):
            m = q % NQ
            nc.vector.scalar_tensor_tensor(out=ends[q][:], in0=ends[q][:], scalar=gain[:, m:m + 1], in1=falls[q][:],
                                           op0=ALU.mult, op1=ALU.mult)

        def make_quad(q):
            m = q % NQ
            height = kappa_gain[:, m - EXACT:m - EXACT + 1] if m >= EXACT else kappa[:, m:m + 1]
            w = work.tile([P, B], F32, name="quad", tag="quad", bufs=3)
            nc.vector.scalar_tensor_tensor(out=w[:], in0=mids[q][:], scalar=height, in1=ends[q][:],
                                           op0=ALU.subtract, op1=ALU.mult)
            quad[q] = w

        def make_diff(q):
            k = q % NQ
            d = work.tile([P, B], F32, name="diff", tag="diff", bufs=4)
            nc.vector.scalar_tensor_tensor(out=d[:], in0=quad[q + 1][:], scalar=neg_inv_d4[:, k:k + 1], in1=quad[q][:],
                                           op0=ALU.mult, op1=ALU.add)
            diff[q] = d

        def make_tilt(q):
            jh, k = divmod(q, NQ)
            product = work.tile([P, B], F32, name="tilt", tag="tilt")
            nc.vector.scalar_tensor_tensor(out=product[:], in0=x_t[jh], scalar=t[:, k:k + 1], in1=diff[q][:],
                                           op0=ALU.subtract, op1=ALU.mult)
            tilt[q] = product

        def basis_sum(q):
            for g in range(2):
                bank = psum.tile([P, PACK, P], F32, name="b_bank", tag="basis")
                for tk in range(PACK):
                    cols = slice(g * PASS + tk * P, g * PASS + (tk + 1) * P)
                    nc.tensor.matmul(bank[:, tk, :], lhsT=quad[q + 1][:, cols], rhs=ident[:], is_transpose=True, start=True, stop=False)
                    nc.tensor.matmul(bank[:, tk, :], lhsT=tilt[q][:, cols], rhs=ident[:], is_transpose=True, start=False, stop=True)
                b_bank[q, g] = bank

        def basis_round(q):
            k = q % NQ
            for g in range(2):
                nc.scalar.activation(out=basis_bf[g][:, :, k, :, :],
                                     in_=b_bank[q, g][:].rearrange("p t (c j) -> p c j t", c=NCHUNK),
                                     func=ACT.Relu, scale=basis_scale[:, k:k + 1], bias=neg_floor[:, k:k + 1])

        def basis_quantise(k0, k1, chunks):
            for c in chunks:
                for g in range(2):
                    codes, scales = basis_mx[g]
                    cols = slice(c * PASS + k0 * JC, c * PASS + k1 * JC)
                    nc.vector.quantize_mx(out=codes[:, cols].bitcast(E4M3), scales=scales[:, cols],
                                          in_=basis_bf[g][:, c, k0:k1, :, :].rearrange("p k j t -> p (k j t)"))

        def p_matmuls(q, tag="p"):
            jh, k = divmod(q, NQ)
            for g in range(2):
                bank = psum.tile([P, PASS], F32, name="p_bank", tag=tag)
                for h in range(2):
                    wc, ws = cp_mx[jh, h]
                    gc, gs = g_feat[h]
                    nc.tensor.matmul_mx(out=bank[:], lhsT=wc[:, k * P:(k + 1) * P].bitcast(E4M3), lhsT_scale=ws[:, k * P:(k + 1) * P],
                                        rhs=gc[:, g * PASS:(g + 1) * PASS].bitcast(E5M2), rhs_scale=gs[:, g * PASS:(g + 1) * PASS],
                                        start=(h == 0), stop=(h == 1))
                p_bank[q, g] = bank

        def dx_term(q, g):
            k = q % NQ
            prod = work.tile([P, PASS], F32, name="prod", tag="prod", bufs=4)
            nc.vector.scalar_tensor_tensor(out=prod[:], in0=diff[q][:, g * PASS:(g + 1) * PASS], scalar=slope_scale[:, k:k + 1],
                                           in1=p_bank[q, g][:], op0=ALU.mult, op1=ALU.mult)
            prods[q, g] = prod

        def dx_add(q, g):
            jh, k = divmod(q, NQ)
            if k == 0:
                bank = psum.tile([P, PACK, P], F32, name="dx_bank", tag="dx")
                dx_bank[jh, g] = bank
            for tk in range(PACK):
                nc.tensor.matmul(dx_bank[jh, g][:, tk, :], lhsT=prods[q, g][:, tk * P:(tk + 1) * P], rhs=ident[:], is_transpose=True,
                                 start=(k == 0 and tk == 0), stop=(k == NK - 1 and tk == PACK - 1))

        def dx_store(jh):
            for g in range(2):
                res = work.tile([P, PACK, P], F32, name="dx_res", tag="dx_res")
                nc.scalar.copy(out=res[:], in_=dx_bank[jh, g][:])
                dst = out_0[g * PASS:(g + 1) * PASS, jh * P:(jh + 1) * P]
                nc.sync.dma_start(out=dst.rearrange("(p t) j -> p t j", t=PACK), in_=res[:])

        n_banks = OUT // P * NCHUNK

        def dcp_matmuls(jh, u, tag):
            ot, c = divmod(u, NCHUNK)
            bank = psum.tile([P, PASS], F32, name="o_bank", tag=tag)
            for g in range(2):
                gc, gs = g_tok[g]
                bc, bs = basis_mx[g]
                nc.tensor.matmul_mx(out=bank[:], lhsT=gc[:, ot * P:(ot + 1) * P].bitcast(E5M2), lhsT_scale=gs[:, ot * P:(ot + 1) * P],
                                    rhs=bc[:, c * PASS:(c + 1) * PASS].bitcast(E4M3), rhs_scale=bs[:, c * PASS:(c + 1) * PASS],
                                    start=(g == 0), stop=(g == 1))
            o_bank[jh, u] = bank

        def dcp_copy(jh, u, copy):
            ot, c = divmod(u, NCHUNK)
            if c == 0:
                if jh == 1 and ot % 2 == 1:
                    res = work.tile([P, P, SLOTS], F32, name="dcp_res", tag="cp_raw", align_bytes=64)
                else:
                    res = work.tile([P, P, SLOTS], F32, name="dcp_res", tag="io", bufs=3)
                dcp_res[jh, ot] = res
            res = dcp_res[jh, ot]
            copy(out=res[:, c * JC:(c + 1) * JC, :], in_=o_bank[jh, u][:, :SLOTS * JC].rearrange("p (k j) -> p j k", j=JC))
            per_store = (NCHUNK, NCHUNK // 2)[jh]
            if (c + 1) % per_store == 0:
                j0, j1 = (c + 1 - per_store) * JC, (c + 1) * JC
                nc.sync.dma_start(out=out_1[ot * P:(ot + 1) * P, jh * P + j0:jh * P + j1, :], in_=res[:, j0:j1, :])

        def dcp_pair(u):
            for v in (u, u + 1):
                if 0 <= v - 2 < n_banks:
                    dcp_copy(0, v - 2, nc.scalar.copy)
                if 0 <= v < n_banks:
                    dcp_matmuls(0, v, "out")

        def is_quad(q):
            return 0 <= q < 2 * NQ

        def is_cubic(q):
            return is_quad(q) and q % NQ < NK

        def dx_of_step(n):
            i = n - FIRST_DX + (n > CATCH_UP)
            return i + i // NK if 0 <= i < 2 * NK else -1

        clamp(0)
        ramp(0)
        square_ends(0)
        square_mid(0)
        nc.vector.tensor_tensor(out=plateau[:, EXACT:], in0=top[:], in1=neg_left[:], op=ALU.add)
        lam_sig = combine("lam_sig", lam[:], sig[:], ALU.mult)
        sig_h = combine("sig_h", sig[:], h_mid, ALU.subtract)
        plateau2 = combine("plateau2", plateau[:], plateau[:], ALU.mult)
        inv_sig2 = combine("inv_sig2", inv_sig[:], inv_sig[:], ALU.mult)
        kap_num = combine("kap_num", sig_h[:], prd[:], ALU.mult)
        den2 = combine("den2", den[:], plateau2[:], ALU.mult)
        clamp(1)
        inv_den = recip("inv_den", den2[:])
        kappa = combine("kappa", kap_num[:], inv_sig2[:], ALU.mult)
        inv_d4 = recip("inv_d4", d4[:])
        gain = combine("gain", lam_sig[:], inv_den[:], ALU.mult)
        inv_lam = recip("inv_lam", lam[:, :NK])
        right = combine("right", high[:], t[:, EXACT + 3:NQ + 3], ALU.subtract)
        root0 = small("root0", NQ - EXACT)
        nc.scalar.activation(out=root0[:], in_=gain[:, EXACT:], func=ACT.Sqrt)
        join_ends(0)
        neg_inv_d4 = scaled("neg_inv_d4", inv_d4[:], -1.0)
        gap = combine("gap", right[:], neg_left[:], ALU.add)
        kappa_gain = combine("kappa_gain", kappa[:, EXACT:], gain[:, EXACT:], ALU.mult)
        basis_scale = scaled("basis_scale", inv_lam[:], -1.0)
        slope_scale = scaled("slope_scale", inv_lam[:], -3.0)
        inv_root0 = recip("inv_root0", root0[:])
        gap2 = combine("gap2", gap[:], gap[:], ALU.mult, nc.gpsimd)
        twice = scaled("twice", inv_lam[:], -2.0, nc.gpsimd)
        nc.gpsimd.tensor_tensor(out=residue[:, EXACT:], in0=gap2[:], in1=kappa_gain[:], op=ALU.mult)
        spread = combine("spread", residue[:, 1:], inv_d4[:], ALU.mult, nc.gpsimd)
        both = combine("both", residue[:, :NK], residue[:, 1:], ALU.add, nc.gpsimd)
        bound = combine("bound", spread[:], both[:], ALU.add, nc.gpsimd)
        neg_floor = combine("neg_floor", bound[:], twice[:], ALU.mult, nc.gpsimd)
        make_quad(0)
        quot = combine("quot", gain[:, EXACT:], inv_root0[:], ALU.mult)
        clamp(2)
        root2 = combine("root2", quot[:], root0[:], ALU.add)
        half_mu = scaled("half_mu", neg_mu[:, EXACT:], 0.5)
        root = scaled("root", root2[:], 0.5)
        mid_bias = combine("mid_bias", half_mu[:], root2[:], ALU.mult)
        nc.scalar.copy(out=x_t[1], in_=x_bank[1])

        for n in range(2 * NQ):
            dx_q = dx_of_step(n)
            u0 = NCHUNK * (n - FIRST_DCP)
            if is_cubic(n - BASIS_LAG):
                basis_sum(n - BASIS_LAG)
            if is_quad(n + 1):
                ramp(n + 1)
            if is_cubic(dx_q):
                dx_term(dx_q, 0)
            if n % NQ < EXACT and n > 0:
                join_ends(n)
            dcp_pair(u0 - 2)
            if is_quad(n + 1):
                square_mid(n + 1)
            if is_cubic(n - SLOPE_LAG):
                make_diff(n - SLOPE_LAG)
            if is_cubic(dx_q):
                dx_term(dx_q, 1)
            if n > 0:
                make_quad(n)
            if is_cubic(n - BASIS_LAG):
                basis_round(n - BASIS_LAG)
            if is_cubic(dx_q):
                dx_add(dx_q, 0)
                dx_add(dx_q, 1)
            if n == CATCH_UP:
                dx_store(0)
                p_matmuls(NQ)
            elif is_cubic(dx_of_step(n + 1)):
                p_matmuls(dx_of_step(n + 1))
            if is_quad(n + 2) and n > 0:
                clamp(n + 2)
            if is_cubic(n - SLOPE_LAG):
                make_tilt(n - SLOPE_LAG)
            dcp_pair(u0)
            if is_quad(n + 1):
                square_ends(n + 1)
            quantise_pending()
            if n == CATCH_UP:
                for g in range(2):
                    dx_term(NQ, g)
                for g in range(2):
                    dx_add(NQ, g)
                p_matmuls(NQ + 1)
            if n in (FIRST_DCP - 3, FIRST_DCP - 2):
                basis_quantise(0, EARLY_K, [n - (FIRST_DCP - 3)])
            if n == FIRST_DCP - 1:
                basis_quantise(0, EARLY_K, [2, 3])
                basis_quantise(EARLY_K, NK, range(NCHUNK))
            if n == 2 * NQ - 1:
                basis_quantise(0, EARLY_K, [0, 1])
            if n < 2:
                make_g_feat(0, n, "dx")
                make_g_feat(1, n, "p")
            if n > 0:
                for i in cp_left[:2 if n in DOUBLE_CP else 1]:
                    make_cp(i)
                    cp_left.remove(i)
            if 0 <= n - FIRST_G_TOK < 2 * G_PIECES:
                make_g_tok(n - FIRST_G_TOK)

        last = 2 * NQ - 2
        basis_sum(last - 1)
        p_matmuls(last, "out")
        make_diff(last)
        basis_round(last - 1)
        basis_quantise(0, EARLY_K, [2])
        make_tilt(last)
        basis_sum(last)
        basis_quantise(0, EARLY_K, [3])
        for q in (last - 1, last):
            for g in range(2):
                dx_term(q, g)
                dx_add(q, g)
        basis_round(last)
        basis_quantise(EARLY_K, NK, range(NCHUNK))
        dx_store(1)

        tags = ("p", "p", "out", "out", "basis", "basis")
        for u in range(len(tags)):
            dcp_matmuls(1, u, tags[u])
        for u in range(n_banks):
            dcp_copy(1, u, nc.vector.tensor_copy if u % 2 == 0 else nc.scalar.copy)
            if u + len(tags) < n_banks:
                dcp_matmuls(1, u + len(tags), tags[u % len(tags)])
